import numpy as np
import ml_dtypes


def mxq(x, axis, fmt="e4m3"):
    dtype, down = {"e4m3": (ml_dtypes.float8_e4m3fn, 7), "e5m2": (ml_dtypes.float8_e5m2, 14)}[fmt]
    v = np.moveaxis(np.asarray(x, np.float32).astype(ml_dtypes.bfloat16).astype(np.float64), axis, -1)
    blocks = v.reshape(v.shape[:-1] + (-1, 32))
    amax = np.abs(blocks).max(-1, keepdims=True)
    byte = np.maximum(np.where(amax > 0, np.frexp(amax)[1] - 1 + 127, 0) - down, 1)
    scale = np.exp2(byte - 127.0)
    codes = (blocks / scale).astype(np.float32).astype(dtype).astype(np.float64)
    return np.moveaxis((codes * scale).reshape(v.shape), -1, axis)


WIDE = False


def mx_kscale(k):
    if not WIDE:
        return np.ones(k)
    levels = np.array([10, -10, 5, -5, 0])
    if k % 512:
        return np.exp2(np.random.permutation(np.resize(levels, k // 32))).repeat(32)
    a = np.empty((k // 512, 16))
    for p in range(k // 512):
        a[p, :8] = np.random.permutation(np.resize(levels, 8))
        for g in range(8):
            far = levels[np.abs(levels - a[p, g]) >= 10]
            a[p, g + 8] = far[np.random.randint(len(far))]
    return np.exp2(a.ravel()).repeat(32)


BF16 = ml_dtypes.bfloat16


def bf(x):
    return np.asarray(x, np.float32).astype(BF16)


def f64(x):
    return np.asarray(x).astype(np.float64)


B, T, D, H, DH, DFF = 4, 2048, 1024, 4, 32, 4096
HD = H * DH
EPS = 1e-5


def layer_norm(x, w):
    mu = x.mean(-1, keepdims=True)
    var = ((x - mu) ** 2).mean(-1, keepdims=True)
    return (x - mu) * (1.0 / np.sqrt(var + EPS)) * w


def setup_inputs():
    s = mx_kscale(D)
    spread = 0.5 + np.random.random((B, T, 1))
    shift = 0.5 * np.random.standard_normal((B, T, 1))
    return {"x": bf(np.random.standard_normal((B, T, D)) * spread + shift),
            "ln1_w": bf((1.0 + 0.1 * np.random.standard_normal(D)) * s),
            "qkv_w": bf(np.random.standard_normal((3 * HD, D)) / np.sqrt(D) / s[None, :])}


def reference(x, ln1_w, qkv_w):
    h = layer_norm(f64(x), f64(ln1_w))
    qkv = mxq(h, 2, "e4m3") @ mxq(f64(qkv_w), 1, "e4m3").T
    qkv = qkv.reshape(B, T, 3, H, DH)
    q = qkv[:, :, 0].transpose(0, 2, 1, 3)
    k = qkv[:, :, 1].transpose(0, 2, 1, 3)
    v = qkv[:, :, 2].transpose(0, 2, 1, 3)
    return q, k, v

@@ -1,0 +1,298 @@
+from contextlib import ExitStack
+
+import concourse.mybir as mybir
+from concourse.masks import make_identity
+
+BF16 = mybir.dt.bfloat16
+F32 = mybir.dt.float32
+U32 = mybir.dt.uint32
+U8 = mybir.dt.uint8
+FP8X4 = mybir.dt.float8_e4m3fn_x4
+ALU = mybir.AluOpType
+ACT = mybir.ActivationFunctionType
+
+BATCH, TOKENS, D = 4, 2048, 1024
+HEADS, DH = 4, 32
+C = 3 * HEADS * DH
+EPS = 1e-5
+
+P = 128
+PACK = 4
+K_PASS = P * PACK
+PASSES = D // K_PASS
+N_PAD = 512
+COLUMN_GROUPS = ((0, 256), (256, C))
+BN_WIDTH = 512
+BN_DIM = 6
+
+ROWS = TOKENS // P
+CHUNK = 4
+HALF = CHUNK // 2
+TILES = BATCH * ROWS
+CHUNKS = TILES // CHUNK
+CHUNKS_PER_BATCH = ROWS // CHUNK
+PREFETCH = 2
+
+DEVIATION_LAG = 1
+NORMALISE_LAG = 5
+GAIN_LAG = NORMALISE_LAG + 1
+QUANTISE_LAG = GAIN_LAG + 1
+TRANSPOSE_AHEAD = 2
+
+FLOPS = 2 * BATCH * TOKENS * D * C
+
+
+def tile_traceableencoderlayer_pa_t_kernel(tc, x, ln1_w, qkv_w, out_0, out_1, out_2):
+    nc = tc.nc
+    outs = (out_0, out_1, out_2)
+
+    with ExitStack() as ctx:
+        const = ctx.enter_context(tc.tile_pool(name="const", bufs=1))
+        x_pool = ctx.enter_context(tc.tile_pool(name="x_pool", bufs=PREFETCH + NORMALISE_LAG + 1))
+        stats = ctx.enter_context(tc.tile_pool(name="stats", bufs=NORMALISE_LAG + 2))
+        scrap = ctx.enter_context(tc.tile_pool(name="scrap", bufs=2))
+        y_pool = ctx.enter_context(tc.tile_pool(name="y_pool", bufs=2 * CHUNK))
+        mx_pool = ctx.enter_context(tc.tile_pool(name="mx_pool", bufs=2))
+        out_pool = ctx.enter_context(tc.tile_pool(name="out_pool", bufs=3))
+        psum_t = ctx.enter_context(tc.psum_pool(name="psum_t", bufs=PASSES * TRANSPOSE_AHEAD))
+        psum_o = ctx.enter_context(tc.psum_pool(name="psum_o", bufs=CHUNK))
+        ctx.enter_context(tc.manual_schedule())
+
+        x_tiles, bn_parts, mean_var, sums, neg_mean, sq_sums, std, rstd = {}, {}, {}, {}, {}, {}, {}, {}
+        y_tiles, turned, grouped, codes, scales, acc, out_tiles = {}, {}, {}, {}, {}, {}, {}
+
+        def load(c):
+            b, q = divmod(c, CHUNKS_PER_BATCH)
+            x_tiles[c] = x_pool.tile([P, CHUNK, D], BF16, name="x_chunk")
+            rows = x[b].rearrange("(p s) k -> p s k", s=ROWS)
+            nc.sync.dma_start(out=x_tiles[c][:], in_=rows[:, q * CHUNK : (q + 1) * CHUNK, :])
+
+        w_raw = const.tile([P, C // P, D], BF16, name="w_raw")
+        nc.sync.dma_start(out=w_raw[:], in_=qkv_w.rearrange("(a p) k -> p a k", p=P))
+        gain_bf = const.tile([P, PASSES, PACK], BF16, name="gain_bf")
+        nc.sync.dma_start(out=gain_bf[:], in_=ln1_w.rearrange("(g p t) -> p g t", p=P, t=PACK))
+        for c in range(PREFETCH):
+            load(c)
+
+        ident_bf = const.tile([P, P], BF16, name="ident_bf")
+        make_identity(nc, ident_bf[:])
+        ident_f32 = const.tile([P, P], F32, name="ident_f32")
+        make_identity(nc, ident_f32[:])
+        eps = const.tile([P, 1], F32, name="eps")
+        nc.vector.memset(eps[:], EPS)
+
+        w_grouped = const.tile([P, PASSES, N_PAD, PACK], BF16, name="w_grouped", align_bytes=64)
+        nc.vector.memset(w_grouped[:], 0.0)
+        w_codes = const.tile([P, PASSES, N_PAD], U32, name="w_codes", align_bytes=64)
+        w_scales = const.tile([P, PASSES, N_PAD], U8, name="w_scales", align_bytes=64)
+        gain_cols = const.tile([P, D // P], F32, name="gain_cols")
+
+        for a in range(C // P):
+            w_turned = psum_t.tile([P, PASSES, PACK, P], BF16, name="w_turned", tag="turned")
+            for g in range(PASSES):
+                for t in range(PACK):
+                    nc.tensor.transpose(
+                        w_turned[:, g, t, :],
+                        w_raw[:, a, g * K_PASS + t : (g + 1) * K_PASS : PACK],
+                        ident_bf[:],
+                    )
+            nc.scalar.copy(
+                out=w_grouped[:, :, a * P : (a + 1) * P, :],
+                in_=w_turned[:].rearrange("p g t c -> p g c t"),
+            )
+        nc.scalar.copy(out=gain_cols[:], in_=gain_bf[:].rearrange("p g t -> p (g t)"))
+
+        def quantise_weights():
+            nc.vector.quantize_mx(
+                out=w_codes[:].rearrange("p g c -> p (g c)").bitcast(FP8X4),
+                scales=w_scales[:].rearrange("p g c -> p (g c)"),
+                in_=w_grouped[:].rearrange("p g c t -> p (g c t)"),
+            )
+
+        def vector_statistics(i):
+            c, j = divmod(i, CHUNK)
+            if j == 0:
+                bn_parts[c] = stats.tile([P, HALF, D // BN_WIDTH, BN_DIM], F32, name="bn_parts")
+            for h in range(D // BN_WIDTH):
+                nc.vector.bn_stats(
+                    out=bn_parts[c][:, j // 2, h, :],
+                    in_=x_tiles[c][:, j, h * BN_WIDTH : (h + 1) * BN_WIDTH],
+                )
+
+        def vector_mean_and_variance(c):
+            mean_var[c] = stats.tile([P, HALF, 2], F32, name="mean_var")
+            for n in range(HALF):
+                nc.vector.bn_aggr(
+                    out=mean_var[c][:, n, :], in_=bn_parts[c][:, n, :, :].rearrange("p h s -> p (h s)")
+                )
+            neg_mean[c, 0] = stats.tile([P, HALF], F32, name="neg_mean_v")
+            nc.vector.tensor_scalar_mul(out=neg_mean[c, 0][:], in0=mean_var[c][:, :, 0], scalar1=-1.0)
+
+        def scalar_sum(i):
+            c, j = divmod(i, CHUNK)
+            if j == 1:
+                sums[c] = stats.tile([P, HALF], F32, name="sums")
+            unread = scrap.tile([P, D], BF16, name="unread")
+            nc.scalar.activation(
+                out=unread[:],
+                in_=x_tiles[c][:, j, :],
+                func=ACT.Identity,
+                accum_out=sums[c][:, j // 2 : j // 2 + 1],
+            )
+
+        def scalar_mean(c):
+            neg_mean[c, 1] = stats.tile([P, HALF], F32, name="neg_mean_s")
+            nc.scalar.mul(out=neg_mean[c, 1][:], in_=sums[c][:], mul=-1.0 / D)
+
+        def scalar_squares(i):
+            c, j = divmod(i, CHUNK)
+            if j == 1:
+                sq_sums[c] = stats.tile([P, HALF], F32, name="sq_sums")
+            unread = scrap.tile([P, D], BF16, name="unread")
+            nc.scalar.activation(
+                out=unread[:],
+                in_=x_tiles[c][:, j, :],
+                func=ACT.Square,
+                bias=neg_mean[c, 1][:, j // 2 : j // 2 + 1],
+                scale=1.0,
+                accum_out=sq_sums[c][:, j // 2 : j // 2 + 1],
+            )
+
+        def deviation(c):
+            std[c] = stats.tile([P, 2, HALF], F32, name="std")
+            nc.scalar.activation(
+                out=std[c][:, 0, :], in_=mean_var[c][:, :, 1], func=ACT.Sqrt, bias=eps[:, 0:1], scale=1.0
+            )
+            nc.scalar.activation(
+                out=std[c][:, 1, :], in_=sq_sums[c][:], func=ACT.Sqrt, bias=eps[:, 0:1], scale=1.0 / D
+            )
+
+        def inverse_deviation(c):
+            rstd[c] = stats.tile([P, 2, HALF], F32, name="rstd")
+            nc.vector.reciprocal(out=rstd[c][:], in_=std[c][:])
+
+        def normalise(i):
+            c, j = divmod(i, CHUNK)
+            y_tiles[i] = y_pool.tile([P, PASSES, PACK, P], F32, name="y")
+            nc.gpsimd.tensor_scalar(
+                out=y_tiles[i][:],
+                in0=x_tiles[c][:, j, :].rearrange("r (g p t) -> r g t p", g=PASSES, t=PACK),
+                scalar1=neg_mean[c, j % 2][:, j // 2 : j // 2 + 1],
+                scalar2=rstd[c][:, j % 2, j // 2 : j // 2 + 1],
+                op0=ALU.add,
+                op1=ALU.mult,
+            )
+
+        def transpose(i):
+            turned[i] = []
+            for g in range(PASSES):
+                bank = psum_t.tile([P, PACK, P], F32, name="turned")
+                for t in range(PACK):
+                    nc.tensor.transpose(bank[:, t, :], y_tiles[i][:, g, t, :], ident_f32[:])
+                turned[i].append(bank)
+
+        def gain(i):
+            c, j = divmod(i, CHUNK)
+            if j == 0:
+                grouped[c] = mx_pool.tile(
+                    [P, CHUNK, PASSES, P, PACK], BF16, name="grouped", align_bytes=64
+                )
+            for g in range(PASSES):
+                nc.vector.tensor_tensor(
+                    out=grouped[c][:, j, g, :, :],
+                    in0=turned[i][g][:].rearrange("p t r -> p r t"),
+                    in1=gain_cols[:, g * PACK : (g + 1) * PACK].unsqueeze(1).to_broadcast([P, P, PACK]),
+                    op=ALU.mult,
+                )
+
+        def quantise(c):
+            codes[c] = mx_pool.tile([P, CHUNK, PASSES, P], U32, name="codes", align_bytes=64)
+            scales[c] = mx_pool.tile([P, CHUNK, PASSES, P], U8, name="scales", align_bytes=64)
+            nc.vector.quantize_mx(
+                out=codes[c][:].rearrange("p j g r -> p (j g r)").bitcast(FP8X4),
+                scales=scales[c][:].rearrange("p j g r -> p (j g r)"),
+                in_=grouped[c][:].rearrange("p j g r t -> p (j g r t)"),
+            )
+
+        def project(c):
+            for j in range(CHUNK):
+                i = c * CHUNK + j
+                acc[i] = psum_o.tile([P, C], F32, name="acc")
+                for lo, hi in COLUMN_GROUPS:
+                    for g in range(PASSES):
+                        nc.tensor.matmul_mx(
+                            out=acc[i][:, lo:hi],
+                            lhsT=codes[c][:, j, g, :].bitcast(FP8X4),
+                            lhsT_scale=scales[c][:, j, g, :],
+                            rhs=w_codes[:, g, lo:hi].bitcast(FP8X4),
+                            rhs_scale=w_scales[:, g, lo:hi],
+                            start=(g == 0),
+                            stop=(g == PASSES - 1),
+                        )
+
+        def copy_out(i):
+            c, j = divmod(i, CHUNK)
+            if j == 0:
+                out_tiles[c] = out_pool.tile([P, 3 * HEADS, CHUNK, DH], F32, name="out_chunk")
+            nc.scalar.copy(
+                out=out_tiles[c][:, :, j, :],
+                in_=acc[i][:].rearrange("p (a d) -> p a d", d=DH),
+            )
+
+        def store(c):
+            b, q = divmod(c, CHUNKS_PER_BATCH)
+            for w in range(3):
+                rows = outs[w][b].rearrange("n (p s) d -> p n s d", s=ROWS)
+                nc.sync.dma_start(
+                    out=rows[:, :, q * CHUNK : (q + 1) * CHUNK, :],
+                    in_=out_tiles[c][:, w * HEADS : (w + 1) * HEADS, :, :],
+                )
+
+        def due(step, lag):
+            c = step - lag
+            return c if 0 <= c < CHUNKS else None
+
+        for step in range(CHUNKS + QUANTISE_LAG):
+            measured = due(step, 0)
+            finished = due(step, DEVIATION_LAG)
+            normalised = due(step, NORMALISE_LAG)
+            gained = due(step, GAIN_LAG)
+            quantised = due(step, QUANTISE_LAG)
+
+            if due(step, -PREFETCH) is not None:
+                load(step + PREFETCH)
+
+            if finished is not None:
+                vector_mean_and_variance(finished)
+                deviation(finished)
+            if quantised == 0:
+                quantise_weights()
+            if quantised is not None:
+                quantise(quantised)
+            if normalised is not None:
+                inverse_deviation(normalised)
+
+            if quantised is not None:
+                project(quantised)
+
+            for j in range(CHUNK):
+                if measured is not None and j % 2 == 0:
+                    vector_statistics(measured * CHUNK + j)
+                if measured is not None and j % 2 == 1:
+                    scalar_sum(measured * CHUNK + j)
+                if normalised is not None:
+                    normalise(normalised * CHUNK + j)
+                if gained is not None:
+                    gain(gained * CHUNK + j)
+                i = (step - GAIN_LAG) * CHUNK + j + TRANSPOSE_AHEAD
+                if 0 <= i < TILES:
+                    transpose(i)
+                if quantised is not None:
+                    copy_out(quantised * CHUNK + j)
+
+            if measured is not None:
+                scalar_mean(measured)
+                for j in range(1, CHUNK, 2):
+                    scalar_squares(measured * CHUNK + j)
+            if quantised is not None:
+                store(quantised)

@@ -21,25 +21,29 @@ PACK = 4
 K_PASS = P * PACK
 PASSES = D // K_PASS
 N_PAD = 512
-COLUMN_GROUPS = ((0, 256), (256, C))
 BN_WIDTH = 512
 BN_DIM = 6
 
 ROWS = TOKENS // P
 CHUNK = 4
-HALF = CHUNK // 2
 TILES = BATCH * ROWS
 CHUNKS = TILES // CHUNK
 CHUNKS_PER_BATCH = ROWS // CHUNK
 PREFETCH = 2
 
-DEVIATION_LAG = 1
-NORMALISE_LAG = 5
-GAIN_LAG = NORMALISE_LAG + 1
+SQUARES_LAG = CHUNK
+RSTD_LAG = 2 * CHUNK
+NORMALISE_LAG = RSTD_LAG + 1
+TRANSPOSE_LAG = NORMALISE_LAG + 1
+GAIN_LAG = TRANSPOSE_LAG + 2
 QUANTISE_LAG = GAIN_LAG + 1
-TRANSPOSE_AHEAD = 2
+COPY_LAG = QUANTISE_LAG + 1
 
 FLOPS = 2 * BATCH * TOKENS * D * C
+
+
+def vector_tiles(c):
+    return CHUNK if c == 0 else 1 + c % 2
 
 
 def tile_traceableencoderlayer_pa_t_kernel(tc, x, ln1_w, qkv_w, out_0, out_1, out_2):
@@ -48,46 +52,55 @@ def tile_traceableencoderlayer_pa_t_kernel(tc, x, ln1_w, qkv_w, out_0, out_1, ou
 
     with ExitStack() as ctx:
         const = ctx.enter_context(tc.tile_pool(name="const", bufs=1))
-        x_pool = ctx.enter_context(tc.tile_pool(name="x_pool", bufs=PREFETCH + NORMALISE_LAG + 1))
-        stats = ctx.enter_context(tc.tile_pool(name="stats", bufs=NORMALISE_LAG + 2))
+        x_pool = ctx.enter_context(tc.tile_pool(name="x_pool", bufs=PREFETCH + 4))
+        stats = ctx.enter_context(tc.tile_pool(name="stats", bufs=4))
         scrap = ctx.enter_context(tc.tile_pool(name="scrap", bufs=2))
-        y_pool = ctx.enter_context(tc.tile_pool(name="y_pool", bufs=2 * CHUNK))
-        mx_pool = ctx.enter_context(tc.tile_pool(name="mx_pool", bufs=2))
+        y_pool = ctx.enter_context(tc.tile_pool(name="y_pool", bufs=5))
+        mx_pool = ctx.enter_context(tc.tile_pool(name="mx_pool", bufs=3))
         out_pool = ctx.enter_context(tc.tile_pool(name="out_pool", bufs=3))
-        psum_t = ctx.enter_context(tc.psum_pool(name="psum_t", bufs=PASSES * TRANSPOSE_AHEAD))
-        psum_o = ctx.enter_context(tc.psum_pool(name="psum_o", bufs=CHUNK))
+        psum_t = ctx.enter_context(tc.psum_pool(name="psum_t", bufs=5))
+        psum_o = ctx.enter_context(tc.psum_pool(name="psum_o", bufs=3))
         ctx.enter_context(tc.manual_schedule())
 
-        x_tiles, bn_parts, mean_var, sums, neg_mean, sq_sums, std, rstd = {}, {}, {}, {}, {}, {}, {}, {}
+        x_tiles, bn_parts, mean_var, sums, moments, std, rstd = {}, {}, {}, {}, {}, {}, {}
         y_tiles, turned, grouped, codes, scales, acc, out_tiles = {}, {}, {}, {}, {}, {}, {}
 
-        def load(c):
+        def load(c, parts=1):
             b, q = divmod(c, CHUNKS_PER_BATCH)
             x_tiles[c] = x_pool.tile([P, CHUNK, D], BF16, name="x_chunk")
             rows = x[b].rearrange("(p s) k -> p s k", s=ROWS)
-            nc.sync.dma_start(out=x_tiles[c][:], in_=rows[:, q * CHUNK : (q + 1) * CHUNK, :])
+            n = CHUNK // parts
+            for part in range(parts):
+                lo = part * n
+                nc.sync.dma_start(
+                    out=x_tiles[c][:, lo : lo + n, :],
+                    in_=rows[:, q * CHUNK + lo : q * CHUNK + lo + n, :],
+                )
 
-        w_raw = const.tile([P, C // P, D], BF16, name="w_raw")
-        nc.sync.dma_start(out=w_raw[:], in_=qkv_w.rearrange("(a p) k -> p a k", p=P))
+        load(0, parts=CHUNK)
         gain_bf = const.tile([P, PASSES, PACK], BF16, name="gain_bf")
         nc.sync.dma_start(out=gain_bf[:], in_=ln1_w.rearrange("(g p t) -> p g t", p=P, t=PACK))
-        for c in range(PREFETCH):
-            load(c)
+        load(1)
+        w_raw = const.tile([P, C // P, D], BF16, name="w_raw")
+        nc.sync.dma_start(out=w_raw[:], in_=qkv_w.rearrange("(a p) k -> p a k", p=P))
 
         ident_bf = const.tile([P, P], BF16, name="ident_bf")
         make_identity(nc, ident_bf[:])
         ident_f32 = const.tile([P, P], F32, name="ident_f32")
         make_identity(nc, ident_f32[:])
         eps = const.tile([P, 1], F32, name="eps")
-        nc.vector.memset(eps[:], EPS)
+        nc.gpsimd.memset(eps[:], EPS)
+        moment_factors = const.tile([P, 2], F32, name="moment_factors")
+        nc.gpsimd.memset(moment_factors[:, 0:1], -1.0)
+        nc.gpsimd.memset(moment_factors[:, 1:2], float(D))
 
         w_grouped = const.tile([P, PASSES, N_PAD, PACK], BF16, name="w_grouped", align_bytes=64)
-        nc.vector.memset(w_grouped[:], 0.0)
+        nc.gpsimd.memset(w_grouped[:, :, C:N_PAD, :], 0.0)
         w_codes = const.tile([P, PASSES, N_PAD], U32, name="w_codes", align_bytes=64)
         w_scales = const.tile([P, PASSES, N_PAD], U8, name="w_scales", align_bytes=64)
-        gain_cols = const.tile([P, D // P], F32, name="gain_cols")
+        gain_cols = const.tile([P, PASSES, PACK], F32, name="gain_cols")
 
-        for a in range(C // P):
+        def group_weights(a):
             w_turned = psum_t.tile([P, PASSES, PACK, P], BF16, name="w_turned", tag="turned")
             for g in range(PASSES):
                 for t in range(PACK):
@@ -100,7 +113,6 @@ def tile_traceableencoderlayer_pa_t_kernel(tc, x, ln1_w, qkv_w, out_0, out_1, ou
                 out=w_grouped[:, :, a * P : (a + 1) * P, :],
                 in_=w_turned[:].rearrange("p g t c -> p g c t"),
             )
-        nc.scalar.copy(out=gain_cols[:], in_=gain_bf[:].rearrange("p g t -> p (g t)"))
 
         def quantise_weights():
             nc.vector.quantize_mx(
@@ -109,66 +121,65 @@ def tile_traceableencoderlayer_pa_t_kernel(tc, x, ln1_w, qkv_w, out_0, out_1, ou
                 in_=w_grouped[:].rearrange("p g c t -> p (g c t)"),
             )
 
-        def vector_statistics(i):
-            c, j = divmod(i, CHUNK)
-            if j == 0:
-                bn_parts[c] = stats.tile([P, HALF, D // BN_WIDTH, BN_DIM], F32, name="bn_parts")
-            for h in range(D // BN_WIDTH):
-                nc.vector.bn_stats(
-                    out=bn_parts[c][:, j // 2, h, :],
-                    in_=x_tiles[c][:, j, h * BN_WIDTH : (h + 1) * BN_WIDTH],
-                )
+        def start_moments(c):
+            moments[c] = stats.tile([P, 2, CHUNK], F32, name="moments")
+            n = vector_tiles(c)
+            bn_parts[c] = stats.tile([P, CHUNK, D // BN_WIDTH, BN_DIM], F32, name="bn_parts")
+            if n < CHUNK:
+                sums[c] = stats.tile([P, CHUNK], F32, name="sums")
 
-        def vector_mean_and_variance(c):
-            mean_var[c] = stats.tile([P, HALF, 2], F32, name="mean_var")
-            for n in range(HALF):
+        def vector_statistics(c, j, h):
+            nc.vector.bn_stats(
+                out=bn_parts[c][:, j, h, :],
+                in_=x_tiles[c][:, j, h * BN_WIDTH : (h + 1) * BN_WIDTH],
+            )
+
+        def vector_moments(c):
+            n = vector_tiles(c)
+            mean_var[c] = stats.tile([P, CHUNK, 2], F32, name="mean_var")
+            for j in range(n):
                 nc.vector.bn_aggr(
-                    out=mean_var[c][:, n, :], in_=bn_parts[c][:, n, :, :].rearrange("p h s -> p (h s)")
+                    out=mean_var[c][:, j, :], in_=bn_parts[c][:, j, :, :].rearrange("p h s -> p (h s)")
                 )
-            neg_mean[c, 0] = stats.tile([P, HALF], F32, name="neg_mean_v")
-            nc.vector.tensor_scalar_mul(out=neg_mean[c, 0][:], in0=mean_var[c][:, :, 0], scalar1=-1.0)
+            nc.vector.tensor_tensor(
+                out=moments[c][:, :, 0:n],
+                in0=mean_var[c][:, 0:n, :].rearrange("p j m -> p m j"),
+                in1=moment_factors[:].unsqueeze(2).to_broadcast([P, 2, n]),
+                op=ALU.mult,
+            )
 
-        def scalar_sum(i):
-            c, j = divmod(i, CHUNK)
-            if j == 1:
-                sums[c] = stats.tile([P, HALF], F32, name="sums")
+        def scalar_sum(c, j):
             unread = scrap.tile([P, D], BF16, name="unread")
             nc.scalar.activation(
                 out=unread[:],
                 in_=x_tiles[c][:, j, :],
                 func=ACT.Identity,
-                accum_out=sums[c][:, j // 2 : j // 2 + 1],
+                accum_out=sums[c][:, j : j + 1],
             )
 
         def scalar_mean(c):
-            neg_mean[c, 1] = stats.tile([P, HALF], F32, name="neg_mean_s")
-            nc.scalar.mul(out=neg_mean[c, 1][:], in_=sums[c][:], mul=-1.0 / D)
+            n = vector_tiles(c)
+            nc.scalar.mul(out=moments[c][:, 0, n:CHUNK], in_=sums[c][:, n:CHUNK], mul=-1.0 / D)
 
-        def scalar_squares(i):
-            c, j = divmod(i, CHUNK)
-            if j == 1:
-                sq_sums[c] = stats.tile([P, HALF], F32, name="sq_sums")
+        def scalar_squares(c, j):
             unread = scrap.tile([P, D], BF16, name="unread")
             nc.scalar.activation(
                 out=unread[:],
                 in_=x_tiles[c][:, j, :],
                 func=ACT.Square,
-                bias=neg_mean[c, 1][:, j // 2 : j // 2 + 1],
+                bias=moments[c][:, 0, j : j + 1],
                 scale=1.0,
-                accum_out=sq_sums[c][:, j // 2 : j // 2 + 1],
+                accum_out=moments[c][:, 1, j : j + 1],
             )
 
         def deviation(c):
-            std[c] = stats.tile([P, 2, HALF], F32, name="std")
+            std[c] = stats.tile([P, CHUNK], F32, name="std")
             nc.scalar.activation(
-                out=std[c][:, 0, :], in_=mean_var[c][:, :, 1], func=ACT.Sqrt, bias=eps[:, 0:1], scale=1.0
-            )
-            nc.scalar.activation(
-                out=std[c][:, 1, :], in_=sq_sums[c][:], func=ACT.Sqrt, bias=eps[:, 0:1], scale=1.0 / D
+                out=std[c][:], in_=moments[c][:, 1, :], func=ACT.Sqrt, bias=eps[:, 0:1], scale=1.0 / D
             )
 
         def inverse_deviation(c):
-            rstd[c] = stats.tile([P, 2, HALF], F32, name="rstd")
+            rstd[c] = stats.tile([P, CHUNK], F32, name="rstd")
             nc.vector.reciprocal(out=rstd[c][:], in_=std[c][:])
 
         def normalise(i):
@@ -177,58 +188,48 @@ def tile_traceableencoderlayer_pa_t_kernel(tc, x, ln1_w, qkv_w, out_0, out_1, ou
             nc.gpsimd.tensor_scalar(
                 out=y_tiles[i][:],
                 in0=x_tiles[c][:, j, :].rearrange("r (g p t) -> r g t p", g=PASSES, t=PACK),
-                scalar1=neg_mean[c, j % 2][:, j // 2 : j // 2 + 1],
-                scalar2=rstd[c][:, j % 2, j // 2 : j // 2 + 1],
+                scalar1=moments[c][:, 0, j : j + 1],
+                scalar2=rstd[c][:, j : j + 1],
                 op0=ALU.add,
                 op1=ALU.mult,
             )
 
-        def transpose(i):
-            turned[i] = []
-            for g in range(PASSES):
-                bank = psum_t.tile([P, PACK, P], F32, name="turned")
-                for t in range(PACK):
-                    nc.tensor.transpose(bank[:, t, :], y_tiles[i][:, g, t, :], ident_f32[:])
-                turned[i].append(bank)
+        def transpose(i, g):
+            turned[i, g] = psum_t.tile([P, PACK, P], F32, name="turned")
+            for t in range(PACK):
+                nc.tensor.transpose(turned[i, g][:, t, :], y_tiles[i][:, g, t, :], ident_f32[:])
 
-        def gain(i):
-            c, j = divmod(i, CHUNK)
-            if j == 0:
-                grouped[c] = mx_pool.tile(
-                    [P, CHUNK, PASSES, P, PACK], BF16, name="grouped", align_bytes=64
-                )
-            for g in range(PASSES):
-                nc.vector.tensor_tensor(
-                    out=grouped[c][:, j, g, :, :],
-                    in0=turned[i][g][:].rearrange("p t r -> p r t"),
-                    in1=gain_cols[:, g * PACK : (g + 1) * PACK].unsqueeze(1).to_broadcast([P, P, PACK]),
-                    op=ALU.mult,
-                )
-
-        def quantise(c):
-            codes[c] = mx_pool.tile([P, CHUNK, PASSES, P], U32, name="codes", align_bytes=64)
-            scales[c] = mx_pool.tile([P, CHUNK, PASSES, P], U8, name="scales", align_bytes=64)
-            nc.vector.quantize_mx(
-                out=codes[c][:].rearrange("p j g r -> p (j g r)").bitcast(FP8X4),
-                scales=scales[c][:].rearrange("p j g r -> p (j g r)"),
-                in_=grouped[c][:].rearrange("p j g r t -> p (j g r t)"),
+        def gain(i, g):
+            if g == 0:
+                grouped[i] = mx_pool.tile([P, PASSES, P, PACK], BF16, name="grouped", align_bytes=64)
+            nc.vector.tensor_tensor(
+                out=grouped[i][:, g, :, :],
+                in0=turned[i, g][:].rearrange("p t r -> p r t"),
+                in1=gain_cols[:, g, :].unsqueeze(1).to_broadcast([P, P, PACK]),
+                op=ALU.mult,
             )
 
-        def project(c):
-            for j in range(CHUNK):
-                i = c * CHUNK + j
-                acc[i] = psum_o.tile([P, C], F32, name="acc")
-                for lo, hi in COLUMN_GROUPS:
-                    for g in range(PASSES):
-                        nc.tensor.matmul_mx(
-                            out=acc[i][:, lo:hi],
-                            lhsT=codes[c][:, j, g, :].bitcast(FP8X4),
-                            lhsT_scale=scales[c][:, j, g, :],
-                            rhs=w_codes[:, g, lo:hi].bitcast(FP8X4),
-                            rhs_scale=w_scales[:, g, lo:hi],
-                            start=(g == 0),
-                            stop=(g == PASSES - 1),
-                        )
+        def quantise(i):
+            codes[i] = mx_pool.tile([P, PASSES, P], U32, name="codes", align_bytes=64)
+            scales[i] = mx_pool.tile([P, PASSES, P], U8, name="scales", align_bytes=64)
+            nc.vector.quantize_mx(
+                out=codes[i][:].rearrange("p g r -> p (g r)").bitcast(FP8X4),
+                scales=scales[i][:].rearrange("p g r -> p (g r)"),
+                in_=grouped[i][:].rearrange("p g r t -> p (g r t)"),
+            )
+
+        def project(i):
+            acc[i] = psum_o.tile([P, N_PAD], F32, name="acc")
+            for g in range(PASSES):
+                nc.tensor.matmul_mx(
+                    out=acc[i][:],
+                    lhsT=codes[i][:, g, :].bitcast(FP8X4),
+                    lhsT_scale=scales[i][:, g, :],
+                    rhs=w_codes[:, g, :].bitcast(FP8X4),
+                    rhs_scale=w_scales[:, g, :],
+                    start=(g == 0),
+                    stop=(g == PASSES - 1),
+                )
 
         def copy_out(i):
             c, j = divmod(i, CHUNK)
@@ -236,7 +237,7 @@ def tile_traceableencoderlayer_pa_t_kernel(tc, x, ln1_w, qkv_w, out_0, out_1, ou
                 out_tiles[c] = out_pool.tile([P, 3 * HEADS, CHUNK, DH], F32, name="out_chunk")
             nc.scalar.copy(
                 out=out_tiles[c][:, :, j, :],
-                in_=acc[i][:].rearrange("p (a d) -> p a d", d=DH),
+                in_=acc[i][:, 0:C].rearrange("p (a d) -> p a d", d=DH),
             )
 
         def store(c):
@@ -249,50 +250,74 @@ def tile_traceableencoderlayer_pa_t_kernel(tc, x, ln1_w, qkv_w, out_0, out_1, ou
                 )
 
         def due(step, lag):
-            c = step - lag
-            return c if 0 <= c < CHUNKS else None
+            i = step - lag
+            return i if 0 <= i < TILES else None
 
-        for step in range(CHUNKS + QUANTISE_LAG):
-            measured = due(step, 0)
-            finished = due(step, DEVIATION_LAG)
+        FIRST_RSTD_STEP = CHUNK + 2
+        WEIGHTS_STEP = FIRST_RSTD_STEP + 1
+
+        for step in range(TILES + COPY_LAG):
+            c, k = divmod(step, CHUNK)
+            measured = due(step, 0) is not None
+            squared = due(step, SQUARES_LAG) is not None
             normalised = due(step, NORMALISE_LAG)
+            turned_now = due(step, TRANSPOSE_LAG)
             gained = due(step, GAIN_LAG)
             quantised = due(step, QUANTISE_LAG)
+            copied = due(step, COPY_LAG)
 
-            if due(step, -PREFETCH) is not None:
-                load(step + PREFETCH)
+            if k == 0 and c + PREFETCH < CHUNKS:
+                load(c + PREFETCH)
+            if measured and k == 0:
+                start_moments(c)
 
-            if finished is not None:
-                vector_mean_and_variance(finished)
-                deviation(finished)
-            if quantised == 0:
+            halves = []
+            if measured:
+                n = vector_tiles(c) * (D // BN_WIDTH)
+                halves = [divmod(m, D // BN_WIDTH) for m in range(n) if m * CHUNK // n == k]
+
+            if squared and k == 0 and vector_tiles(c - 1) < CHUNK:
+                scalar_mean(c - 1)
+            if measured and k >= vector_tiles(c):
+                scalar_sum(c, k)
+            if copied is not None:
+                copy_out(copied)
+            if WEIGHTS_STEP <= step < WEIGHTS_STEP + C // P:
+                group_weights(step - WEIGHTS_STEP)
+            if squared and k + vector_tiles(c - 1) < CHUNK:
+                scalar_squares(c - 1, k + vector_tiles(c - 1))
+            if step == FIRST_RSTD_STEP:
+                deviation(0)
+            if k == 0 and due(step, RSTD_LAG) is not None and c > 2:
+                deviation(c - 2)
+
+            if gained is not None:
+                gain(gained, 0)
+            if step == FIRST_RSTD_STEP:
+                inverse_deviation(0)
+            if k == 1 and due(step, NORMALISE_LAG) is not None and c > 2:
+                inverse_deviation(c - 2)
+            for j, h in halves[0::2]:
+                vector_statistics(c, j, h)
+            if step == GAIN_LAG - 2:
+                nc.vector.tensor_copy(out=gain_cols[:], in_=gain_bf[:])
                 quantise_weights()
             if quantised is not None:
                 quantise(quantised)
-            if normalised is not None:
-                inverse_deviation(normalised)
+            if gained is not None:
+                gain(gained, 1)
+            for j, h in halves[1::2]:
+                vector_statistics(c, j, h)
+            if squared and k == 0:
+                vector_moments(c - 1)
 
+            if normalised is not None:
+                normalise(normalised)
+
+            if turned_now is not None:
+                for g in range(PASSES):
+                    transpose(turned_now, g)
             if quantised is not None:
                 project(quantised)
-
-            for j in range(CHUNK):
-                if measured is not None and j % 2 == 0:
-                    vector_statistics(measured * CHUNK + j)
-                if measured is not None and j % 2 == 1:
-                    scalar_sum(measured * CHUNK + j)
-                if normalised is not None:
-                    normalise(normalised * CHUNK + j)
-                if gained is not None:
-                    gain(gained * CHUNK + j)
-                i = (step - GAIN_LAG) * CHUNK + j + TRANSPOSE_AHEAD
-                if 0 <= i < TILES:
-                    transpose(i)
-                if quantised is not None:
-                    copy_out(quantised * CHUNK + j)
-
-            if measured is not None:
-                scalar_mean(measured)
-                for j in range(1, CHUNK, 2):
-                    scalar_squares(measured * CHUNK + j)
-            if quantised is not None:
-                store(quantised)
+            if copied is not None and copied % CHUNK == CHUNK - 1:
+                store(copied // CHUNK)

@@ -36,14 +36,15 @@ RSTD_LAG = 2 * CHUNK
 NORMALISE_LAG = RSTD_LAG + 1
 TRANSPOSE_LAG = NORMALISE_LAG + 1
 GAIN_LAG = TRANSPOSE_LAG + 2
-QUANTISE_LAG = GAIN_LAG + 1
+QUANTISE_LAG = GAIN_LAG + CHUNK + 1
+LAST_QUANTISE_LAG = GAIN_LAG + 1
 COPY_LAG = QUANTISE_LAG + 1
 
 FLOPS = 2 * BATCH * TOKENS * D * C
 
 
 def vector_tiles(c):
-    return CHUNK if c == 0 else 1 + c % 2
+    return CHUNK - 1 if c == 0 else 1 + c % 2
 
 
 def tile_traceableencoderlayer_pa_t_kernel(tc, x, ln1_w, qkv_w, out_0, out_1, out_2):
@@ -80,9 +81,9 @@ def tile_traceableencoderlayer_pa_t_kernel(tc, x, ln1_w, qkv_w, out_0, out_1, ou
         load(0, parts=CHUNK)
         gain_bf = const.tile([P, PASSES, PACK], BF16, name="gain_bf")
         nc.sync.dma_start(out=gain_bf[:], in_=ln1_w.rearrange("(g p t) -> p g t", p=P, t=PACK))
-        load(1)
         w_raw = const.tile([P, C // P, D], BF16, name="w_raw")
         nc.sync.dma_start(out=w_raw[:], in_=qkv_w.rearrange("(a p) k -> p a k", p=P))
+        load(1)
 
         ident_bf = const.tile([P, P], BF16, name="ident_bf")
         make_identity(nc, ident_bf[:])
@@ -200,31 +201,33 @@ def tile_traceableencoderlayer_pa_t_kernel(tc, x, ln1_w, qkv_w, out_0, out_1, ou
                 nc.tensor.transpose(turned[i, g][:, t, :], y_tiles[i][:, g, t, :], ident_f32[:])
 
         def gain(i, g):
-            if g == 0:
-                grouped[i] = mx_pool.tile([P, PASSES, P, PACK], BF16, name="grouped", align_bytes=64)
+            c, j = divmod(i, CHUNK)
+            if j == 0 and g == 0:
+                grouped[c] = mx_pool.tile([P, CHUNK, PASSES, P, PACK], BF16, name="grouped", align_bytes=64)
+                codes[c] = mx_pool.tile([P, CHUNK, PASSES, P], U32, name="codes", align_bytes=64)
+                scales[c] = mx_pool.tile([P, CHUNK, PASSES, P], U8, name="scales", align_bytes=64)
             nc.vector.tensor_tensor(
-                out=grouped[i][:, g, :, :],
+                out=grouped[c][:, j, g, :, :],
                 in0=turned[i, g][:].rearrange("p t r -> p r t"),
                 in1=gain_cols[:, g, :].unsqueeze(1).to_broadcast([P, P, PACK]),
                 op=ALU.mult,
             )
 
-        def quantise(i):
-            codes[i] = mx_pool.tile([P, PASSES, P], U32, name="codes", align_bytes=64)
-            scales[i] = mx_pool.tile([P, PASSES, P], U8, name="scales", align_bytes=64)
+        def quantise(c, lo, hi):
             nc.vector.quantize_mx(
-                out=codes[i][:].rearrange("p g r -> p (g r)").bitcast(FP8X4),
-                scales=scales[i][:].rearrange("p g r -> p (g r)"),
-                in_=grouped[i][:].rearrange("p g r t -> p (g r t)"),
+                out=codes[c][:, lo:hi, :, :].rearrange("p j g r -> p (j g r)").bitcast(FP8X4),
+                scales=scales[c][:, lo:hi, :, :].rearrange("p j g r -> p (j g r)"),
+                in_=grouped[c][:, lo:hi, :, :, :].rearrange("p j g r t -> p (j g r t)"),
             )
 
         def project(i):
+            c, j = divmod(i, CHUNK)
             acc[i] = psum_o.tile([P, N_PAD], F32, name="acc")
             for g in range(PASSES):
                 nc.tensor.matmul_mx(
                     out=acc[i][:],
-                    lhsT=codes[i][:, g, :].bitcast(FP8X4),
-                    lhsT_scale=scales[i][:, g, :],
+                    lhsT=codes[c][:, j, g, :].bitcast(FP8X4),
+                    lhsT_scale=scales[c][:, j, g, :],
                     rhs=w_codes[:, g, :].bitcast(FP8X4),
                     rhs_scale=w_scales[:, g, :],
                     start=(g == 0),
@@ -253,7 +256,10 @@ def tile_traceableencoderlayer_pa_t_kernel(tc, x, ln1_w, qkv_w, out_0, out_1, ou
             i = step - lag
             return i if 0 <= i < TILES else None
 
-        FIRST_RSTD_STEP = CHUNK + 2
+        def project_lag(i):
+            return QUANTISE_LAG if i < TILES - CHUNK else LAST_QUANTISE_LAG + 1
+
+        FIRST_RSTD_STEP = CHUNK + 1
         WEIGHTS_STEP = FIRST_RSTD_STEP + 1
 
         for step in range(TILES + COPY_LAG):
@@ -263,8 +269,8 @@ def tile_traceableencoderlayer_pa_t_kernel(tc, x, ln1_w, qkv_w, out_0, out_1, ou
             normalised = due(step, NORMALISE_LAG)
             turned_now = due(step, TRANSPOSE_LAG)
             gained = due(step, GAIN_LAG)
-            quantised = due(step, QUANTISE_LAG)
-            copied = due(step, COPY_LAG)
+            projected = [i for i in range(TILES) if i + project_lag(i) == step]
+            copied = [i for i in range(TILES) if i + project_lag(i) + 1 == step]
 
             if k == 0 and c + PREFETCH < CHUNKS:
                 load(c + PREFETCH)
@@ -280,8 +286,8 @@ def tile_traceableencoderlayer_pa_t_kernel(tc, x, ln1_w, qkv_w, out_0, out_1, ou
                 scalar_mean(c - 1)
             if measured and k >= vector_tiles(c):
                 scalar_sum(c, k)
-            if copied is not None:
-                copy_out(copied)
+            for i in copied:
+                copy_out(i)
             if WEIGHTS_STEP <= step < WEIGHTS_STEP + C // P:
                 group_weights(step - WEIGHTS_STEP)
             if squared and k + vector_tiles(c - 1) < CHUNK:
@@ -295,15 +301,19 @@ def tile_traceableencoderlayer_pa_t_kernel(tc, x, ln1_w, qkv_w, out_0, out_1, ou
                 gain(gained, 0)
             if step == FIRST_RSTD_STEP:
                 inverse_deviation(0)
+                nc.vector.tensor_copy(out=gain_cols[:], in_=gain_bf[:])
+            if due(step, QUANTISE_LAG) is not None and due(step, QUANTISE_LAG) % CHUNK == 0:
+                if due(step, QUANTISE_LAG) < TILES - CHUNK:
+                    quantise(due(step, QUANTISE_LAG) // CHUNK, 0, CHUNK)
+            if due(step, LAST_QUANTISE_LAG) is not None and due(step, LAST_QUANTISE_LAG) >= TILES - CHUNK:
+                j = due(step, LAST_QUANTISE_LAG) % CHUNK
+                quantise(CHUNKS - 1, j, j + 1)
             if k == 1 and due(step, NORMALISE_LAG) is not None and c > 2:
                 inverse_deviation(c - 2)
             for j, h in halves[0::2]:
                 vector_statistics(c, j, h)
-            if step == GAIN_LAG - 2:
-                nc.vector.tensor_copy(out=gain_cols[:], in_=gain_bf[:])
+            if step == QUANTISE_LAG - 1:
                 quantise_weights()
-            if quantised is not None:
-                quantise(quantised)
             if gained is not None:
                 gain(gained, 1)
             for j, h in halves[1::2]:
@@ -317,7 +327,8 @@ def tile_traceableencoderlayer_pa_t_kernel(tc, x, ln1_w, qkv_w, out_0, out_1, ou
             if turned_now is not None:
                 for g in range(PASSES):
                     transpose(turned_now, g)
-            if quantised is not None:
-                project(quantised)
-            if copied is not None and copied % CHUNK == CHUNK - 1:
-                store(copied // CHUNK)
+            for i in projected:
+                project(i)
+            for i in copied:
+                if i % CHUNK == CHUNK - 1:
+                    store(i // CHUNK)

@@ -31,9 +31,8 @@ CHUNKS = TILES // CHUNK
 CHUNKS_PER_BATCH = ROWS // CHUNK
 PREFETCH = 2
 
-SQUARES_LAG = CHUNK
-RSTD_LAG = 2 * CHUNK
-NORMALISE_LAG = RSTD_LAG + 1
+MOMENTS_LAG = CHUNK
+NORMALISE_LAG = MOMENTS_LAG + CHUNK - 1
 TRANSPOSE_LAG = NORMALISE_LAG + 1
 GAIN_LAG = TRANSPOSE_LAG + 2
 QUANTISE_LAG = GAIN_LAG + CHUNK + 1
@@ -44,7 +43,7 @@ FLOPS = 2 * BATCH * TOKENS * D * C
 
 
 def vector_tiles(c):
-    return CHUNK - 1 if c == 0 else 1 + c % 2
+    return CHUNK - 1 if c < 2 else 1 + c % 2
 
 
 def tile_traceableencoderlayer_pa_t_kernel(tc, x, ln1_w, qkv_w, out_0, out_1, out_2):
@@ -63,7 +62,7 @@ def tile_traceableencoderlayer_pa_t_kernel(tc, x, ln1_w, qkv_w, out_0, out_1, ou
         psum_o = ctx.enter_context(tc.psum_pool(name="psum_o", bufs=3))
         ctx.enter_context(tc.manual_schedule())
 
-        x_tiles, bn_parts, mean_var, sums, moments, std, rstd = {}, {}, {}, {}, {}, {}, {}
+        x_tiles, bn_parts, moments, neg_mean, std, rstd = {}, {}, {}, {}, {}, {}
         y_tiles, turned, grouped, codes, scales, acc, out_tiles = {}, {}, {}, {}, {}, {}, {}
 
         def load(c, parts=1):
@@ -91,9 +90,8 @@ def tile_traceableencoderlayer_pa_t_kernel(tc, x, ln1_w, qkv_w, out_0, out_1, ou
         make_identity(nc, ident_f32[:])
         eps = const.tile([P, 1], F32, name="eps")
         nc.gpsimd.memset(eps[:], EPS)
-        moment_factors = const.tile([P, 2], F32, name="moment_factors")
-        nc.gpsimd.memset(moment_factors[:, 0:1], -1.0)
-        nc.gpsimd.memset(moment_factors[:, 1:2], float(D))
+        sqrt_first = const.tile([P, 1], F32, name="sqrt_first")
+        nc.scalar.activation(out=sqrt_first[:], in_=eps[:], func=ACT.Sqrt)
 
         w_grouped = const.tile([P, PASSES, N_PAD, PACK], BF16, name="w_grouped", align_bytes=64)
         nc.gpsimd.memset(w_grouped[:, :, C:N_PAD, :], 0.0)
@@ -123,11 +121,8 @@ def tile_traceableencoderlayer_pa_t_kernel(tc, x, ln1_w, qkv_w, out_0, out_1, ou
             )
 
         def start_moments(c):
-            moments[c] = stats.tile([P, 2, CHUNK], F32, name="moments")
-            n = vector_tiles(c)
+            moments[c] = stats.tile([P, CHUNK, 2], F32, name="moments")
             bn_parts[c] = stats.tile([P, CHUNK, D // BN_WIDTH, BN_DIM], F32, name="bn_parts")
-            if n < CHUNK:
-                sums[c] = stats.tile([P, CHUNK], F32, name="sums")
 
         def vector_statistics(c, j, h):
             nc.vector.bn_stats(
@@ -136,31 +131,20 @@ def tile_traceableencoderlayer_pa_t_kernel(tc, x, ln1_w, qkv_w, out_0, out_1, ou
             )
 
         def vector_moments(c):
-            n = vector_tiles(c)
-            mean_var[c] = stats.tile([P, CHUNK, 2], F32, name="mean_var")
-            for j in range(n):
+            for j in range(vector_tiles(c)):
                 nc.vector.bn_aggr(
-                    out=mean_var[c][:, j, :], in_=bn_parts[c][:, j, :, :].rearrange("p h s -> p (h s)")
+                    out=moments[c][:, j, :], in_=bn_parts[c][:, j, :, :].rearrange("p h s -> p (h s)")
                 )
-            nc.vector.tensor_tensor(
-                out=moments[c][:, :, 0:n],
-                in0=mean_var[c][:, 0:n, :].rearrange("p j m -> p m j"),
-                in1=moment_factors[:].unsqueeze(2).to_broadcast([P, 2, n]),
-                op=ALU.mult,
-            )
 
-        def scalar_sum(c, j):
+        def scalar_mean(c, j):
             unread = scrap.tile([P, D], BF16, name="unread")
             nc.scalar.activation(
                 out=unread[:],
                 in_=x_tiles[c][:, j, :],
                 func=ACT.Identity,
-                accum_out=sums[c][:, j : j + 1],
+                scale=-1.0 / D,
+                accum_out=moments[c][:, j, 0:1],
             )
-
-        def scalar_mean(c):
-            n = vector_tiles(c)
-            nc.scalar.mul(out=moments[c][:, 0, n:CHUNK], in_=sums[c][:, n:CHUNK], mul=-1.0 / D)
 
         def scalar_squares(c, j):
             unread = scrap.tile([P, D], BF16, name="unread")
@@ -168,28 +152,47 @@ def tile_traceableencoderlayer_pa_t_kernel(tc, x, ln1_w, qkv_w, out_0, out_1, ou
                 out=unread[:],
                 in_=x_tiles[c][:, j, :],
                 func=ACT.Square,
-                bias=moments[c][:, 0, j : j + 1],
+                bias=moments[c][:, j, 0:1],
                 scale=1.0,
-                accum_out=moments[c][:, 1, j : j + 1],
+                accum_out=moments[c][:, j, 1:2],
             )
 
         def deviation(c):
+            n = vector_tiles(c)
             std[c] = stats.tile([P, CHUNK], F32, name="std")
-            nc.scalar.activation(
-                out=std[c][:], in_=moments[c][:, 1, :], func=ACT.Sqrt, bias=eps[:, 0:1], scale=1.0 / D
-            )
+            for lo, hi, factor in ((0, n, 1.0), (n, CHUNK, 1.0 / D)):
+                nc.scalar.activation(
+                    out=std[c][:, lo:hi],
+                    in_=moments[c][:, lo:hi, 1],
+                    func=ACT.Sqrt,
+                    bias=eps[:, 0:1],
+                    scale=factor,
+                )
 
         def inverse_deviation(c):
             rstd[c] = stats.tile([P, CHUNK], F32, name="rstd")
             nc.vector.reciprocal(out=rstd[c][:], in_=std[c][:])
 
+        def negate_means(c):
+            n = vector_tiles(c)
+            neg_mean[c] = stats.tile([P, CHUNK], F32, name="neg_mean")
+            nc.gpsimd.tensor_scalar(
+                out=neg_mean[c][:, 0:n],
+                in0=moments[c][:, 0:n, 0],
+                scalar1=-1.0,
+                scalar2=0.0,
+                op0=ALU.mult,
+                op1=ALU.add,
+            )
+
         def normalise(i):
             c, j = divmod(i, CHUNK)
+            shift = neg_mean[c][:, j : j + 1] if j < vector_tiles(c) else moments[c][:, j, 0:1]
             y_tiles[i] = y_pool.tile([P, PASSES, PACK, P], F32, name="y")
             nc.gpsimd.tensor_scalar(
                 out=y_tiles[i][:],
                 in0=x_tiles[c][:, j, :].rearrange("r (g p t) -> r g t p", g=PASSES, t=PACK),
-                scalar1=moments[c][:, 0, j : j + 1],
+                scalar1=shift,
                 scalar2=rstd[c][:, j : j + 1],
                 op0=ALU.add,
                 op1=ALU.mult,
@@ -202,7 +205,7 @@ def tile_traceableencoderlayer_pa_t_kernel(tc, x, ln1_w, qkv_w, out_0, out_1, ou
 
         def gain(i, g):
             c, j = divmod(i, CHUNK)
-            if j == 0 and g == 0:
+            if j == 0 and g == 1:
                 grouped[c] = mx_pool.tile([P, CHUNK, PASSES, P, PACK], BF16, name="grouped", align_bytes=64)
                 codes[c] = mx_pool.tile([P, CHUNK, PASSES, P], U32, name="codes", align_bytes=64)
                 scales[c] = mx_pool.tile([P, CHUNK, PASSES, P], U8, name="scales", align_bytes=64)
@@ -259,16 +262,29 @@ def tile_traceableencoderlayer_pa_t_kernel(tc, x, ln1_w, qkv_w, out_0, out_1, ou
         def project_lag(i):
             return QUANTISE_LAG if i < TILES - CHUNK else LAST_QUANTISE_LAG + 1
 
-        FIRST_RSTD_STEP = CHUNK + 1
-        WEIGHTS_STEP = FIRST_RSTD_STEP + 1
+        def spread(work, k):
+            return [w for m, w in enumerate(work) if m * CHUNK // len(work) == k]
+
+        def scalar_work(c):
+            tiles = range(vector_tiles(c), CHUNK)
+            means = [(scalar_mean, j) for j in tiles]
+            squares = [(scalar_squares, j) for j in tiles]
+            work = means[:2]
+            for mean, square in zip(means[2:], squares):
+                work += [square, mean]
+            return work + squares[len(means[2:]) :]
+
+        WEIGHTS_STEP = NORMALISE_LAG
 
         for step in range(TILES + COPY_LAG):
             c, k = divmod(step, CHUNK)
             measured = due(step, 0) is not None
-            squared = due(step, SQUARES_LAG) is not None
+            finished = due(step, MOMENTS_LAG) is not None and k == 0
             normalised = due(step, NORMALISE_LAG)
             turned_now = due(step, TRANSPOSE_LAG)
             gained = due(step, GAIN_LAG)
+            quantised = due(step, QUANTISE_LAG)
+            quantised_last = due(step, LAST_QUANTISE_LAG)
             projected = [i for i in range(TILES) if i + project_lag(i) == step]
             copied = [i for i in range(TILES) if i + project_lag(i) + 1 == step]
 
@@ -276,52 +292,46 @@ def tile_traceableencoderlayer_pa_t_kernel(tc, x, ln1_w, qkv_w, out_0, out_1, ou
                 load(c + PREFETCH)
             if measured and k == 0:
                 start_moments(c)
-
-            halves = []
-            if measured:
-                n = vector_tiles(c) * (D // BN_WIDTH)
-                halves = [divmod(m, D // BN_WIDTH) for m in range(n) if m * CHUNK // n == k]
-
-            if squared and k == 0 and vector_tiles(c - 1) < CHUNK:
-                scalar_mean(c - 1)
-            if measured and k >= vector_tiles(c):
-                scalar_sum(c, k)
-            for i in copied:
-                copy_out(i)
-            if WEIGHTS_STEP <= step < WEIGHTS_STEP + C // P:
-                group_weights(step - WEIGHTS_STEP)
-            if squared and k + vector_tiles(c - 1) < CHUNK:
-                scalar_squares(c - 1, k + vector_tiles(c - 1))
-            if step == FIRST_RSTD_STEP:
-                deviation(0)
-            if k == 0 and due(step, RSTD_LAG) is not None and c > 2:
-                deviation(c - 2)
+            halves = [divmod(m, 2) for m in range(2 * vector_tiles(c))]
+            halves = spread(halves, k) if measured else []
 
             if gained is not None:
-                gain(gained, 0)
-            if step == FIRST_RSTD_STEP:
-                inverse_deviation(0)
-                nc.vector.tensor_copy(out=gain_cols[:], in_=gain_bf[:])
-            if due(step, QUANTISE_LAG) is not None and due(step, QUANTISE_LAG) % CHUNK == 0:
-                if due(step, QUANTISE_LAG) < TILES - CHUNK:
-                    quantise(due(step, QUANTISE_LAG) // CHUNK, 0, CHUNK)
-            if due(step, LAST_QUANTISE_LAG) is not None and due(step, LAST_QUANTISE_LAG) >= TILES - CHUNK:
-                j = due(step, LAST_QUANTISE_LAG) % CHUNK
+                gain(gained, 1)
+            if finished:
+                vector_moments(c - 1)
+            if quantised is not None and quantised % CHUNK == 0 and quantised < TILES - CHUNK:
+                quantise(quantised // CHUNK, 0, CHUNK)
+            if quantised_last is not None and quantised_last >= TILES - CHUNK:
+                j = quantised_last % CHUNK
                 quantise(CHUNKS - 1, j, j + 1)
-            if k == 1 and due(step, NORMALISE_LAG) is not None and c > 2:
-                inverse_deviation(c - 2)
+            if normalised is not None and normalised % CHUNK == 0:
+                inverse_deviation(normalised // CHUNK)
+            if normalised == 0:
+                nc.vector.tensor_copy(out=gain_cols[:], in_=gain_bf[:])
             for j, h in halves[0::2]:
                 vector_statistics(c, j, h)
             if step == QUANTISE_LAG - 1:
                 quantise_weights()
             if gained is not None:
-                gain(gained, 1)
+                gain(gained, 0)
             for j, h in halves[1::2]:
                 vector_statistics(c, j, h)
-            if squared and k == 0:
-                vector_moments(c - 1)
+
+            passes = spread(scalar_work(c), k) if measured else []
+            for scalar_pass, j in passes[0::2]:
+                scalar_pass(c, j)
+            for i in copied:
+                copy_out(i)
+            if WEIGHTS_STEP <= step < WEIGHTS_STEP + C // P:
+                group_weights(step - WEIGHTS_STEP)
+            for scalar_pass, j in passes[1::2]:
+                scalar_pass(c, j)
+            if finished:
+                deviation(c - 1)
 
             if normalised is not None:
+                if normalised % CHUNK == 0:
+                    negate_means(normalised // CHUNK)
                 normalise(normalised)
 
             if turned_now is not None:

@@ -43,7 +43,13 @@ FLOPS = 2 * BATCH * TOKENS * D * C
 
 
 def vector_tiles(c):
-    return CHUNK - 1 if c < 2 else 1 + c % 2
+    return CHUNK - 1 if c < 2 else 1
+
+
+def tensor_tiles(c):
+    if c < 3:
+        return []
+    return [2, 3] if c % 2 and c < CHUNKS - 1 else [3]
 
 
 def tile_traceableencoderlayer_pa_t_kernel(tc, x, ln1_w, qkv_w, out_0, out_1, out_2):
@@ -58,36 +64,37 @@ def tile_traceableencoderlayer_pa_t_kernel(tc, x, ln1_w, qkv_w, out_0, out_1, ou
         y_pool = ctx.enter_context(tc.tile_pool(name="y_pool", bufs=5))
         mx_pool = ctx.enter_context(tc.tile_pool(name="mx_pool", bufs=3))
         out_pool = ctx.enter_context(tc.tile_pool(name="out_pool", bufs=3))
-        psum_t = ctx.enter_context(tc.psum_pool(name="psum_t", bufs=5))
+        psum_t = ctx.enter_context(tc.psum_pool(name="psum_t", bufs=4))
         psum_o = ctx.enter_context(tc.psum_pool(name="psum_o", bufs=3))
+        psum_s = ctx.enter_context(tc.psum_pool(name="psum_s", bufs=1))
         ctx.enter_context(tc.manual_schedule())
 
-        x_tiles, bn_parts, moments, neg_mean, std, rstd = {}, {}, {}, {}, {}, {}
+        x_tiles, bn_parts, moments, neg_mean, std, rstd, folded = {}, {}, {}, {}, {}, {}, {}
         y_tiles, turned, grouped, codes, scales, acc, out_tiles = {}, {}, {}, {}, {}, {}, {}
 
-        def load(c, parts=1):
+        def load(c, parts=((0, CHUNK),)):
             b, q = divmod(c, CHUNKS_PER_BATCH)
             x_tiles[c] = x_pool.tile([P, CHUNK, D], BF16, name="x_chunk")
             rows = x[b].rearrange("(p s) k -> p s k", s=ROWS)
-            n = CHUNK // parts
-            for part in range(parts):
-                lo = part * n
+            for lo, hi in parts:
                 nc.sync.dma_start(
-                    out=x_tiles[c][:, lo : lo + n, :],
-                    in_=rows[:, q * CHUNK + lo : q * CHUNK + lo + n, :],
+                    out=x_tiles[c][:, lo:hi, :],
+                    in_=rows[:, q * CHUNK + lo : q * CHUNK + hi, :],
                 )
 
-        load(0, parts=CHUNK)
+        load(0, parts=((0, 1), (3, 4), (1, 2), (2, 3)))
         gain_bf = const.tile([P, PASSES, PACK], BF16, name="gain_bf")
         nc.sync.dma_start(out=gain_bf[:], in_=ln1_w.rearrange("(g p t) -> p g t", p=P, t=PACK))
+        load(1)
         w_raw = const.tile([P, C // P, D], BF16, name="w_raw")
         nc.sync.dma_start(out=w_raw[:], in_=qkv_w.rearrange("(a p) k -> p a k", p=P))
-        load(1)
 
         ident_bf = const.tile([P, P], BF16, name="ident_bf")
         make_identity(nc, ident_bf[:])
         ident_f32 = const.tile([P, P], F32, name="ident_f32")
         make_identity(nc, ident_f32[:])
+        ones = const.tile([P, 1], F32, name="ones")
+        nc.gpsimd.memset(ones[:], 1.0)
         eps = const.tile([P, 1], F32, name="eps")
         nc.gpsimd.memset(eps[:], EPS)
         sqrt_first = const.tile([P, 1], F32, name="sqrt_first")
@@ -100,18 +107,20 @@ def tile_traceableencoderlayer_pa_t_kernel(tc, x, ln1_w, qkv_w, out_0, out_1, ou
         gain_cols = const.tile([P, PASSES, PACK], F32, name="gain_cols")
 
         def group_weights(a):
-            w_turned = psum_t.tile([P, PASSES, PACK, P], BF16, name="w_turned", tag="turned")
+            w_turned = psum_t.tile([P, PASSES, 2, P], F32, name="w_turned", tag="turned")
+            words = w_raw[:, a, :].bitcast(F32)
             for g in range(PASSES):
-                for t in range(PACK):
+                for u in range(2):
                     nc.tensor.transpose(
-                        w_turned[:, g, t, :],
-                        w_raw[:, a, g * K_PASS + t : (g + 1) * K_PASS : PACK],
-                        ident_bf[:],
+                        w_turned[:, g, u, :],
+                        words[:, g * K_PASS // 2 + u : (g + 1) * K_PASS // 2 : 2],
+                        ident_f32[:],
                     )
-            nc.scalar.copy(
-                out=w_grouped[:, :, a * P : (a + 1) * P, :],
-                in_=w_turned[:].rearrange("p g t c -> p g c t"),
-            )
+            for g in range(PASSES):
+                nc.scalar.copy(
+                    out=w_grouped[:, g, a * P : (a + 1) * P, :].rearrange("p c t -> p (c t)").bitcast(F32),
+                    in_=w_turned[:, g, :, :].rearrange("p u c -> p c u"),
+                )
 
         def quantise_weights():
             nc.vector.quantize_mx(
@@ -135,6 +144,30 @@ def tile_traceableencoderlayer_pa_t_kernel(tc, x, ln1_w, qkv_w, out_0, out_1, ou
                 nc.vector.bn_aggr(
                     out=moments[c][:, j, :], in_=bn_parts[c][:, j, :, :].rearrange("p h s -> p (h s)")
                 )
+
+        tensor_sums = psum_s.tile([P, P + CHUNK], F32, name="tensor_sums")
+
+        def tensor_fold(c, j):
+            for b in range(D // P):
+                nc.tensor.matmul(
+                    out=tensor_sums[:, 0:P],
+                    lhsT=x_tiles[c][:, j, b * P : (b + 1) * P],
+                    rhs=ident_bf[:],
+                    start=(b == 0),
+                    stop=(b == D // P - 1),
+                )
+
+        def copy_fold(c, j):
+            folded[c, j] = stats.tile([P, P], F32, name="folded")
+            nc.scalar.copy(out=folded[c, j][:], in_=tensor_sums[:, 0:P])
+
+        def tensor_sum(c, j):
+            nc.tensor.matmul(
+                out=tensor_sums[:, P + j : P + j + 1], lhsT=folded[c, j][:], rhs=ones[:], start=True, stop=True
+            )
+
+        def tensor_mean(c, lo):
+            nc.scalar.mul(out=moments[c][:, lo:CHUNK, 0], in_=tensor_sums[:, P + lo : P + CHUNK], mul=-1.0 / D)
 
         def scalar_mean(c, j):
             unread = scrap.tile([P, D], BF16, name="unread")
@@ -266,13 +299,15 @@ def tile_traceableencoderlayer_pa_t_kernel(tc, x, ln1_w, qkv_w, out_0, out_1, ou
             return [w for m, w in enumerate(work) if m * CHUNK // len(work) == k]
 
         def scalar_work(c):
-            tiles = range(vector_tiles(c), CHUNK)
-            means = [(scalar_mean, j) for j in tiles]
-            squares = [(scalar_squares, j) for j in tiles]
+            own = [j for j in range(vector_tiles(c), CHUNK) if j not in tensor_tiles(c)]
+            means = [(scalar_mean, j) for j in own]
+            squares = [(scalar_squares, j) for j in own]
+            late = [(scalar_squares, j) for j in tensor_tiles(c)]
             work = means[:2]
             for mean, square in zip(means[2:], squares):
                 work += [square, mean]
-            return work + squares[len(means[2:]) :]
+            squares = squares[len(means[2:]) :]
+            return work + squares[:1] + late + squares[1:]
 
         WEIGHTS_STEP = NORMALISE_LAG
 
@@ -295,6 +330,9 @@ def tile_traceableencoderlayer_pa_t_kernel(tc, x, ln1_w, qkv_w, out_0, out_1, ou
             halves = [divmod(m, 2) for m in range(2 * vector_tiles(c))]
             halves = spread(halves, k) if measured else []
 
+            here = tensor_tiles(c) if measured else []
+            ahead = tensor_tiles(c + 1) if c + 1 < CHUNKS else []
+
             if gained is not None:
                 gain(gained, 1)
             if finished:
@@ -304,10 +342,8 @@ def tile_traceableencoderlayer_pa_t_kernel(tc, x, ln1_w, qkv_w, out_0, out_1, ou
             if quantised_last is not None and quantised_last >= TILES - CHUNK:
                 j = quantised_last % CHUNK
                 quantise(CHUNKS - 1, j, j + 1)
-            if normalised is not None and normalised % CHUNK == 0:
+            if normalised is not None and normalised % CHUNK == 0 and normalised > 0:
                 inverse_deviation(normalised // CHUNK)
-            if normalised == 0:
-                nc.vector.tensor_copy(out=gain_cols[:], in_=gain_bf[:])
             for j, h in halves[0::2]:
                 vector_statistics(c, j, h)
             if step == QUANTISE_LAG - 1:
@@ -316,7 +352,17 @@ def tile_traceableencoderlayer_pa_t_kernel(tc, x, ln1_w, qkv_w, out_0, out_1, ou
                 gain(gained, 0)
             for j, h in halves[1::2]:
                 vector_statistics(c, j, h)
+            if step == MOMENTS_LAG:
+                deviation(0)
+                nc.vector.tensor_copy(out=gain_cols[:], in_=gain_bf[:])
+                inverse_deviation(0)
 
+            if measured and k == 2 and tensor_tiles(c):
+                tensor_mean(c, tensor_tiles(c)[0])
+            if k == 2 and ahead:
+                copy_fold(c + 1, ahead[0])
+            if k == 0 and here[1:]:
+                copy_fold(c, here[1])
             passes = spread(scalar_work(c), k) if measured else []
             for scalar_pass, j in passes[0::2]:
                 scalar_pass(c, j)
@@ -326,7 +372,7 @@ def tile_traceableencoderlayer_pa_t_kernel(tc, x, ln1_w, qkv_w, out_0, out_1, ou
                 group_weights(step - WEIGHTS_STEP)
             for scalar_pass, j in passes[1::2]:
                 scalar_pass(c, j)
-            if finished:
+            if finished and c > 1:
                 deviation(c - 1)
 
             if normalised is not None:
@@ -339,6 +385,14 @@ def tile_traceableencoderlayer_pa_t_kernel(tc, x, ln1_w, qkv_w, out_0, out_1, ou
                     transpose(turned_now, g)
             for i in projected:
                 project(i)
+            if k == 1 and here[1:]:
+                tensor_sum(c, here[1])
+            if k == 1 and ahead:
+                tensor_fold(c + 1, ahead[0])
+            if k == 3 and ahead:
+                tensor_sum(c + 1, ahead[0])
+            if k == 3 and ahead[1:]:
+                tensor_fold(c + 1, ahead[1])
             for i in copied:
                 if i % CHUNK == CHUNK - 1:
                     store(i // CHUNK)

@@ -43,13 +43,13 @@ FLOPS = 2 * BATCH * TOKENS * D * C
 
 
 def vector_tiles(c):
+    if c == CHUNKS - 1:
+        return 0
     return CHUNK - 1 if c < 2 else 1
 
 
 def tensor_tiles(c):
-    if c < 3:
-        return []
-    return [2, 3] if c % 2 and c < CHUNKS - 1 else [3]
+    return [] if c < 3 else [2, 3] if c % 2 and c > 3 else [3]
 
 
 def tile_traceableencoderlayer_pa_t_kernel(tc, x, ln1_w, qkv_w, out_0, out_1, out_2):
@@ -59,7 +59,7 @@ def tile_traceableencoderlayer_pa_t_kernel(tc, x, ln1_w, qkv_w, out_0, out_1, ou
     with ExitStack() as ctx:
         const = ctx.enter_context(tc.tile_pool(name="const", bufs=1))
         x_pool = ctx.enter_context(tc.tile_pool(name="x_pool", bufs=PREFETCH + 4))
-        stats = ctx.enter_context(tc.tile_pool(name="stats", bufs=4))
+        stats = ctx.enter_context(tc.tile_pool(name="stats", bufs=5))
         scrap = ctx.enter_context(tc.tile_pool(name="scrap", bufs=2))
         y_pool = ctx.enter_context(tc.tile_pool(name="y_pool", bufs=5))
         mx_pool = ctx.enter_context(tc.tile_pool(name="mx_pool", bufs=3))
@@ -69,7 +69,7 @@ def tile_traceableencoderlayer_pa_t_kernel(tc, x, ln1_w, qkv_w, out_0, out_1, ou
         psum_s = ctx.enter_context(tc.psum_pool(name="psum_s", bufs=1))
         ctx.enter_context(tc.manual_schedule())
 
-        x_tiles, bn_parts, moments, neg_mean, std, rstd, folded = {}, {}, {}, {}, {}, {}, {}
+        x_tiles, bn_parts, moments, neg_mean, std, rstd = {}, {}, {}, {}, {}, {}
         y_tiles, turned, grouped, codes, scales, acc, out_tiles = {}, {}, {}, {}, {}, {}, {}
 
         def load(c, parts=((0, CHUNK),)):
@@ -93,8 +93,6 @@ def tile_traceableencoderlayer_pa_t_kernel(tc, x, ln1_w, qkv_w, out_0, out_1, ou
         make_identity(nc, ident_bf[:])
         ident_f32 = const.tile([P, P], F32, name="ident_f32")
         make_identity(nc, ident_f32[:])
-        ones = const.tile([P, 1], F32, name="ones")
-        nc.gpsimd.memset(ones[:], 1.0)
         eps = const.tile([P, 1], F32, name="eps")
         nc.gpsimd.memset(eps[:], EPS)
         sqrt_first = const.tile([P, 1], F32, name="sqrt_first")
@@ -131,7 +129,10 @@ def tile_traceableencoderlayer_pa_t_kernel(tc, x, ln1_w, qkv_w, out_0, out_1, ou
 
         def start_moments(c):
             moments[c] = stats.tile([P, CHUNK, 2], F32, name="moments")
-            bn_parts[c] = stats.tile([P, CHUNK, D // BN_WIDTH, BN_DIM], F32, name="bn_parts")
+            std[c] = stats.tile([P, CHUNK], F32, name="std")
+            rstd[c] = stats.tile([P, CHUNK], F32, name="rstd")
+            if vector_tiles(c) > 0:
+                bn_parts[c] = stats.tile([P, CHUNK, D // BN_WIDTH, BN_DIM], F32, name="bn_parts")
 
         def vector_statistics(c, j, h):
             nc.vector.bn_stats(
@@ -145,29 +146,27 @@ def tile_traceableencoderlayer_pa_t_kernel(tc, x, ln1_w, qkv_w, out_0, out_1, ou
                     out=moments[c][:, j, :], in_=bn_parts[c][:, j, :, :].rearrange("p h s -> p (h s)")
                 )
 
-        tensor_sums = psum_s.tile([P, P + CHUNK], F32, name="tensor_sums")
+        folded = psum_s.tile([P, P], F32, name="folded")
 
         def tensor_fold(c, j):
             for b in range(D // P):
                 nc.tensor.matmul(
-                    out=tensor_sums[:, 0:P],
-                    lhsT=x_tiles[c][:, j, b * P : (b + 1) * P],
-                    rhs=ident_bf[:],
+                    out=folded[:],
+                    lhsT=ident_bf[:],
+                    rhs=x_tiles[c][:, j, b * P : (b + 1) * P],
                     start=(b == 0),
                     stop=(b == D // P - 1),
                 )
 
-        def copy_fold(c, j):
-            folded[c, j] = stats.tile([P, P], F32, name="folded")
-            nc.scalar.copy(out=folded[c, j][:], in_=tensor_sums[:, 0:P])
-
-        def tensor_sum(c, j):
-            nc.tensor.matmul(
-                out=tensor_sums[:, P + j : P + j + 1], lhsT=folded[c, j][:], rhs=ones[:], start=True, stop=True
+        def folded_mean(c, j):
+            unread = scrap.tile([P, D], BF16, name="unread")
+            nc.scalar.activation(
+                out=unread[:, 0:P],
+                in_=folded[:],
+                func=ACT.Identity,
+                scale=-1.0 / D,
+                accum_out=moments[c][:, j, 0:1],
             )
-
-        def tensor_mean(c, lo):
-            nc.scalar.mul(out=moments[c][:, lo:CHUNK, 0], in_=tensor_sums[:, P + lo : P + CHUNK], mul=-1.0 / D)
 
         def scalar_mean(c, j):
             unread = scrap.tile([P, D], BF16, name="unread")
@@ -190,21 +189,22 @@ def tile_traceableencoderlayer_pa_t_kernel(tc, x, ln1_w, qkv_w, out_0, out_1, ou
                 accum_out=moments[c][:, j, 1:2],
             )
 
+        def scalar_deviation(c, lo, hi, factor):
+            nc.scalar.activation(
+                out=std[c][:, lo:hi],
+                in_=moments[c][:, lo:hi, 1],
+                func=ACT.Sqrt,
+                bias=eps[:, 0:1],
+                scale=factor,
+            )
+
         def deviation(c):
             n = vector_tiles(c)
-            std[c] = stats.tile([P, CHUNK], F32, name="std")
-            for lo, hi, factor in ((0, n, 1.0), (n, CHUNK, 1.0 / D)):
-                nc.scalar.activation(
-                    out=std[c][:, lo:hi],
-                    in_=moments[c][:, lo:hi, 1],
-                    func=ACT.Sqrt,
-                    bias=eps[:, 0:1],
-                    scale=factor,
-                )
+            scalar_deviation(c, 0, n, 1.0)
+            scalar_deviation(c, n, CHUNK, 1.0 / D)
 
-        def inverse_deviation(c):
-            rstd[c] = stats.tile([P, CHUNK], F32, name="rstd")
-            nc.vector.reciprocal(out=rstd[c][:], in_=std[c][:])
+        def inverse_deviation(c, lo=0, hi=CHUNK):
+            nc.vector.reciprocal(out=rstd[c][:, lo:hi], in_=std[c][:, lo:hi])
 
         def negate_means(c):
             n = vector_tiles(c)
@@ -301,15 +301,19 @@ def tile_traceableencoderlayer_pa_t_kernel(tc, x, ln1_w, qkv_w, out_0, out_1, ou
         def scalar_work(c):
             own = [j for j in range(vector_tiles(c), CHUNK) if j not in tensor_tiles(c)]
             means = [(scalar_mean, j) for j in own]
-            squares = [(scalar_squares, j) for j in own]
-            late = [(scalar_squares, j) for j in tensor_tiles(c)]
-            work = means[:2]
-            for mean, square in zip(means[2:], squares):
-                work += [square, mean]
-            squares = squares[len(means[2:]) :]
-            return work + squares[:1] + late + squares[1:]
+            squares = [(scalar_squares, j) for j in tensor_tiles(c)[:1]]
+            work = []
+            for mean, j in zip(means, own):
+                work += [mean] + squares[:1]
+                squares = squares[1:] + [(scalar_squares, j)]
+            return work + squares + [(scalar_squares, j) for j in tensor_tiles(c)[1:]]
 
         WEIGHTS_STEP = NORMALISE_LAG
+        LAST = CHUNKS - 1
+
+        def last_tile(step, lag):
+            i = due(step, lag)
+            return [i % CHUNK] if i is not None and i // CHUNK == LAST else []
 
         for step in range(TILES + COPY_LAG):
             c, k = divmod(step, CHUNK)
@@ -325,13 +329,14 @@ def tile_traceableencoderlayer_pa_t_kernel(tc, x, ln1_w, qkv_w, out_0, out_1, ou
 
             if k == 0 and c + PREFETCH < CHUNKS:
                 load(c + PREFETCH)
-            if measured and k == 0:
-                start_moments(c)
+            if step == 0:
+                start_moments(0)
+            if k == 1 and c + 1 < CHUNKS:
+                start_moments(c + 1)
+            ahead = tensor_tiles(c + 1) if c + 1 < CHUNKS else []
+            here = tensor_tiles(c) if c < CHUNKS else []
             halves = [divmod(m, 2) for m in range(2 * vector_tiles(c))]
             halves = spread(halves, k) if measured else []
-
-            here = tensor_tiles(c) if measured else []
-            ahead = tensor_tiles(c + 1) if c + 1 < CHUNKS else []
 
             if gained is not None:
                 gain(gained, 1)
@@ -342,8 +347,10 @@ def tile_traceableencoderlayer_pa_t_kernel(tc, x, ln1_w, qkv_w, out_0, out_1, ou
             if quantised_last is not None and quantised_last >= TILES - CHUNK:
                 j = quantised_last % CHUNK
                 quantise(CHUNKS - 1, j, j + 1)
-            if normalised is not None and normalised % CHUNK == 0 and normalised > 0:
+            if normalised is not None and normalised % CHUNK == 0 and 0 < normalised < LAST * CHUNK:
                 inverse_deviation(normalised // CHUNK)
+            for j in last_tile(step, NORMALISE_LAG):
+                inverse_deviation(LAST, j, j + 1)
             for j, h in halves[0::2]:
                 vector_statistics(c, j, h)
             if step == QUANTISE_LAG - 1:
@@ -357,26 +364,30 @@ def tile_traceableencoderlayer_pa_t_kernel(tc, x, ln1_w, qkv_w, out_0, out_1, ou
                 nc.vector.tensor_copy(out=gain_cols[:], in_=gain_bf[:])
                 inverse_deviation(0)
 
-            if measured and k == 2 and tensor_tiles(c):
-                tensor_mean(c, tensor_tiles(c)[0])
             if k == 2 and ahead:
-                copy_fold(c + 1, ahead[0])
+                folded_mean(c + 1, ahead[0])
             if k == 0 and here[1:]:
-                copy_fold(c, here[1])
-            passes = spread(scalar_work(c), k) if measured else []
+                folded_mean(c, here[1])
+            passes = spread(scalar_work(c), k) if measured and c < LAST else []
+            for j in last_tile(step, NORMALISE_LAG - 2):
+                scalar_deviation(LAST, j, j + 1, 1.0 if j < vector_tiles(LAST) else 1.0 / D)
+            singles = range(vector_tiles(LAST), CHUNK)
+            passes += [(scalar_squares, j) for j in last_tile(step, NORMALISE_LAG - 3) if j in singles]
+            singles = [j for j in singles if j not in tensor_tiles(LAST)]
+            passes += [(scalar_mean, j) for j in last_tile(step, NORMALISE_LAG - 4) if j in singles]
             for scalar_pass, j in passes[0::2]:
-                scalar_pass(c, j)
+                scalar_pass(min(c, LAST), j)
             for i in copied:
                 copy_out(i)
             if WEIGHTS_STEP <= step < WEIGHTS_STEP + C // P:
                 group_weights(step - WEIGHTS_STEP)
             for scalar_pass, j in passes[1::2]:
-                scalar_pass(c, j)
-            if finished and c > 1:
+                scalar_pass(min(c, LAST), j)
+            if finished and 1 < c <= LAST:
                 deviation(c - 1)
 
             if normalised is not None:
-                if normalised % CHUNK == 0:
+                if normalised % CHUNK == 0 and vector_tiles(normalised // CHUNK) > 0:
                     negate_means(normalised // CHUNK)
                 normalise(normalised)
 
@@ -385,12 +396,8 @@ def tile_traceableencoderlayer_pa_t_kernel(tc, x, ln1_w, qkv_w, out_0, out_1, ou
                     transpose(turned_now, g)
             for i in projected:
                 project(i)
-            if k == 1 and here[1:]:
-                tensor_sum(c, here[1])
             if k == 1 and ahead:
                 tensor_fold(c + 1, ahead[0])
-            if k == 3 and ahead:
-                tensor_sum(c + 1, ahead[0])
             if k == 3 and ahead[1:]:
                 tensor_fold(c + 1, ahead[1])
             for i in copied:

@@ -64,9 +64,8 @@ def tile_traceableencoderlayer_pa_t_kernel(tc, x, ln1_w, qkv_w, out_0, out_1, ou
         y_pool = ctx.enter_context(tc.tile_pool(name="y_pool", bufs=5))
         mx_pool = ctx.enter_context(tc.tile_pool(name="mx_pool", bufs=3))
         out_pool = ctx.enter_context(tc.tile_pool(name="out_pool", bufs=3))
-        psum_t = ctx.enter_context(tc.psum_pool(name="psum_t", bufs=4))
+        psum_t = ctx.enter_context(tc.psum_pool(name="psum_t", bufs=5))
         psum_o = ctx.enter_context(tc.psum_pool(name="psum_o", bufs=3))
-        psum_s = ctx.enter_context(tc.psum_pool(name="psum_s", bufs=1))
         ctx.enter_context(tc.manual_schedule())
 
         x_tiles, bn_parts, moments, neg_mean, std, rstd = {}, {}, {}, {}, {}, {}
@@ -146,12 +145,13 @@ def tile_traceableencoderlayer_pa_t_kernel(tc, x, ln1_w, qkv_w, out_0, out_1, ou
                     out=moments[c][:, j, :], in_=bn_parts[c][:, j, :, :].rearrange("p h s -> p (h s)")
                 )
 
-        folded = psum_s.tile([P, P], F32, name="folded")
+        folded = {}
 
-        def tensor_fold(c, j):
+        def tensor_fold(c, j, bank):
+            folded[c, j] = bank[:, C:N_PAD]
             for b in range(D // P):
                 nc.tensor.matmul(
-                    out=folded[:],
+                    out=folded[c, j],
                     lhsT=ident_bf[:],
                     rhs=x_tiles[c][:, j, b * P : (b + 1) * P],
                     start=(b == 0),
@@ -162,7 +162,7 @@ def tile_traceableencoderlayer_pa_t_kernel(tc, x, ln1_w, qkv_w, out_0, out_1, ou
             unread = scrap.tile([P, D], BF16, name="unread")
             nc.scalar.activation(
                 out=unread[:, 0:P],
-                in_=folded[:],
+                in_=folded[c, j],
                 func=ACT.Identity,
                 scale=-1.0 / D,
                 accum_out=moments[c][:, j, 0:1],
@@ -200,7 +200,8 @@ def tile_traceableencoderlayer_pa_t_kernel(tc, x, ln1_w, qkv_w, out_0, out_1, ou
 
         def deviation(c):
             n = vector_tiles(c)
-            scalar_deviation(c, 0, n, 1.0)
+            if n > 0:
+                scalar_deviation(c, 0, n, 1.0)
             scalar_deviation(c, n, CHUNK, 1.0 / D)
 
         def inverse_deviation(c, lo=0, hi=CHUNK):
@@ -396,10 +397,9 @@ def tile_traceableencoderlayer_pa_t_kernel(tc, x, ln1_w, qkv_w, out_0, out_1, ou
                     transpose(turned_now, g)
             for i in projected:
                 project(i)
-            if k == 1 and ahead:
-                tensor_fold(c + 1, ahead[0])
-            if k == 3 and ahead[1:]:
-                tensor_fold(c + 1, ahead[1])
+            for j in ahead[:1] if k == 1 else ahead[1:] if k == 3 else []:
+                bank = acc[projected[0]] if projected else psum_o.tile([P, N_PAD], F32, name="acc")
+                tensor_fold(c + 1, j, bank)
             for i in copied:
                 if i % CHUNK == CHUNK - 1:
                     store(i // CHUNK)

@@ -20,6 +20,8 @@ P = 128
 PACK = 4
 K_PASS = P * PACK
 PASSES = D // K_PASS
+RUN = 8
+SLOTS = PASSES * PACK
 N_PAD = 512
 BN_WIDTH = 512
 BN_DIM = 6
@@ -82,8 +84,12 @@ def tile_traceableencoderlayer_pa_t_kernel(tc, x, ln1_w, qkv_w, out_0, out_1, ou
                 )
 
         load(0, parts=((0, 1), (3, 4), (1, 2), (2, 3)))
-        gain_bf = const.tile([P, PASSES, PACK], BF16, name="gain_bf")
-        nc.sync.dma_start(out=gain_bf[:], in_=ln1_w.rearrange("(g p t) -> p g t", p=P, t=PACK))
+        gain_rows = const.tile([P, P], BF16, name="gain_rows")
+        nc.gpsimd.memset(gain_rows[:], 0.0)
+        nc.sync.dma_start(
+            out=gain_rows[0:SLOTS, :].rearrange("m (b r) -> m b r", r=RUN),
+            in_=ln1_w.rearrange("(b m r) -> m b r", m=SLOTS, r=RUN),
+        )
         load(1)
         w_raw = const.tile([P, C // P, D], BF16, name="w_raw")
         nc.sync.dma_start(out=w_raw[:], in_=qkv_w.rearrange("(a p) k -> p a k", p=P))
@@ -103,21 +109,24 @@ def tile_traceableencoderlayer_pa_t_kernel(tc, x, ln1_w, qkv_w, out_0, out_1, ou
         w_scales = const.tile([P, PASSES, N_PAD], U8, name="w_scales", align_bytes=64)
         gain_cols = const.tile([P, PASSES, PACK], F32, name="gain_cols")
 
-        def group_weights(a):
-            w_turned = psum_t.tile([P, PASSES, 2, P], F32, name="w_turned", tag="turned")
-            words = w_raw[:, a, :].bitcast(F32)
-            for g in range(PASSES):
-                for u in range(2):
-                    nc.tensor.transpose(
-                        w_turned[:, g, u, :],
-                        words[:, g * K_PASS // 2 + u : (g + 1) * K_PASS // 2 : 2],
-                        ident_f32[:],
-                    )
-            for g in range(PASSES):
+        w_slots = const.tile([P, C // P, SLOTS, P], BF16, name="w_slots")
+
+        def sort_weights():
+            for a in range(C // P):
                 nc.scalar.copy(
-                    out=w_grouped[:, g, a * P : (a + 1) * P, :].rearrange("p c t -> p (c t)").bitcast(F32),
-                    in_=w_turned[:, g, :, :].rearrange("p u c -> p c u"),
+                    out=w_slots[:, a, :, :].rearrange("c m (b r) -> c m b r", r=RUN),
+                    in_=w_raw[:, a, :].rearrange("c (b m r) -> c m b r", m=SLOTS, r=RUN),
                 )
+
+        def group_weights(a):
+            w_turned = psum_t.tile([P, PASSES, PACK, P], BF16, name="w_turned", tag="turned")
+            for g in range(PASSES):
+                for t in range(PACK):
+                    nc.tensor.transpose(w_turned[:, g, t, :], w_slots[:, a, PACK * g + t, :], ident_bf[:])
+            nc.scalar.copy(
+                out=w_grouped[:, :, a * P : (a + 1) * P, :],
+                in_=w_turned[:].rearrange("p g t c -> p g c t"),
+            )
 
         def quantise_weights():
             nc.vector.quantize_mx(
@@ -201,6 +210,7 @@ def tile_traceableencoderlayer_pa_t_kernel(tc, x, ln1_w, qkv_w, out_0, out_1, ou
         def deviation(c):
             n = vector_tiles(c)
             if n > 0:
+                negate_means(c)
                 scalar_deviation(c, 0, n, 1.0)
             scalar_deviation(c, n, CHUNK, 1.0 / D)
 
@@ -210,22 +220,15 @@ def tile_traceableencoderlayer_pa_t_kernel(tc, x, ln1_w, qkv_w, out_0, out_1, ou
         def negate_means(c):
             n = vector_tiles(c)
             neg_mean[c] = stats.tile([P, CHUNK], F32, name="neg_mean")
-            nc.gpsimd.tensor_scalar(
-                out=neg_mean[c][:, 0:n],
-                in0=moments[c][:, 0:n, 0],
-                scalar1=-1.0,
-                scalar2=0.0,
-                op0=ALU.mult,
-                op1=ALU.add,
-            )
+            nc.scalar.mul(out=neg_mean[c][:, 0:n], in_=moments[c][:, 0:n, 0], mul=-1.0)
 
         def normalise(i):
             c, j = divmod(i, CHUNK)
             shift = neg_mean[c][:, j : j + 1] if j < vector_tiles(c) else moments[c][:, j, 0:1]
             y_tiles[i] = y_pool.tile([P, PASSES, PACK, P], F32, name="y")
             nc.gpsimd.tensor_scalar(
-                out=y_tiles[i][:],
-                in0=x_tiles[c][:, j, :].rearrange("r (g p t) -> r g t p", g=PASSES, t=PACK),
+                out=y_tiles[i][:].rearrange("p g t (b r) -> p (g t) b r", r=RUN),
+                in0=x_tiles[c][:, j, :].rearrange("p (b m r) -> p m b r", m=SLOTS, r=RUN),
                 scalar1=shift,
                 scalar2=rstd[c][:, j : j + 1],
                 op0=ALU.add,
@@ -309,7 +312,7 @@ def tile_traceableencoderlayer_pa_t_kernel(tc, x, ln1_w, qkv_w, out_0, out_1, ou
                 squares = squares[1:] + [(scalar_squares, j)]
             return work + squares + [(scalar_squares, j) for j in tensor_tiles(c)[1:]]
 
-        WEIGHTS_STEP = NORMALISE_LAG
+        WEIGHTS_STEP = NORMALISE_LAG + 2
         LAST = CHUNKS - 1
 
         def last_tile(step, lag):
@@ -362,7 +365,9 @@ def tile_traceableencoderlayer_pa_t_kernel(tc, x, ln1_w, qkv_w, out_0, out_1, ou
                 vector_statistics(c, j, h)
             if step == MOMENTS_LAG:
                 deviation(0)
-                nc.vector.tensor_copy(out=gain_cols[:], in_=gain_bf[:])
+                gain_turned = psum_t.tile([P, P], BF16, name="gain_turned", tag="turned")
+                nc.tensor.transpose(gain_turned[:], gain_rows[:], ident_bf[:])
+                nc.vector.tensor_copy(out=gain_cols[:].rearrange("p g t -> p (g t)"), in_=gain_turned[:, 0:SLOTS])
                 inverse_deviation(0)
 
             if k == 2 and ahead:
@@ -380,6 +385,8 @@ def tile_traceableencoderlayer_pa_t_kernel(tc, x, ln1_w, qkv_w, out_0, out_1, ou
                 scalar_pass(min(c, LAST), j)
             for i in copied:
                 copy_out(i)
+            if step == WEIGHTS_STEP - 2:
+                sort_weights()
             if WEIGHTS_STEP <= step < WEIGHTS_STEP + C // P:
                 group_weights(step - WEIGHTS_STEP)
             for scalar_pass, j in passes[1::2]:
@@ -388,8 +395,6 @@ def tile_traceableencoderlayer_pa_t_kernel(tc, x, ln1_w, qkv_w, out_0, out_1, ou
                 deviation(c - 1)
 
             if normalised is not None:
-                if normalised % CHUNK == 0 and vector_tiles(normalised // CHUNK) > 0:
-                    negate_means(normalised // CHUNK)
                 normalise(normalised)
 
             if turned_now is not None:

@@ -47,7 +47,7 @@ FLOPS = 2 * BATCH * TOKENS * D * C
 def vector_tiles(c):
     if c == CHUNKS - 1:
         return 0
-    return CHUNK - 1 if c < 2 else 1
+    return CHUNK - 1 if c < 2 else 2 if c == 2 else 1
 
 
 def tensor_tiles(c):
@@ -119,7 +119,7 @@ def tile_traceableencoderlayer_pa_t_kernel(tc, x, ln1_w, qkv_w, out_0, out_1, ou
                 )
 
         def group_weights(a):
-            w_turned = psum_t.tile([P, PASSES, PACK, P], BF16, name="w_turned", tag="turned")
+            w_turned = psum_o.tile([P, PASSES, PACK, P], BF16, name="w_turned", tag="acc")
             for g in range(PASSES):
                 for t in range(PACK):
                     nc.tensor.transpose(w_turned[:, g, t, :], w_slots[:, a, PACK * g + t, :], ident_bf[:])
@@ -297,7 +297,7 @@ def tile_traceableencoderlayer_pa_t_kernel(tc, x, ln1_w, qkv_w, out_0, out_1, ou
             return i if 0 <= i < TILES else None
 
         def project_lag(i):
-            return QUANTISE_LAG if i < TILES - CHUNK else LAST_QUANTISE_LAG + 1
+            return QUANTISE_LAG if i < TILES - 2 * CHUNK else LAST_QUANTISE_LAG + 1
 
         def spread(work, k):
             return [w for m, w in enumerate(work) if m * CHUNK // len(work) == k]
@@ -346,8 +346,11 @@ def tile_traceableencoderlayer_pa_t_kernel(tc, x, ln1_w, qkv_w, out_0, out_1, ou
                 gain(gained, 1)
             if finished:
                 vector_moments(c - 1)
-            if quantised is not None and quantised % CHUNK == 0 and quantised < TILES - CHUNK:
+            if quantised is not None and quantised % CHUNK == 0 and quantised < TILES - 2 * CHUNK:
                 quantise(quantised // CHUNK, 0, CHUNK)
+            if step - LAST_QUANTISE_LAG - 1 in (TILES - 2 * CHUNK, TILES - 2 * CHUNK + 2):
+                j = (step - LAST_QUANTISE_LAG - 1) % CHUNK
+                quantise(CHUNKS - 2, j, j + 2)
             if quantised_last is not None and quantised_last >= TILES - CHUNK:
                 j = quantised_last % CHUNK
                 quantise(CHUNKS - 1, j, j + 1)
@@ -397,11 +400,15 @@ def tile_traceableencoderlayer_pa_t_kernel(tc, x, ln1_w, qkv_w, out_0, out_1, ou
             if normalised is not None:
                 normalise(normalised)
 
+            if step >= 68:
+                for i in projected:
+                    project(i)
             if turned_now is not None:
                 for g in range(PASSES):
                     transpose(turned_now, g)
-            for i in projected:
-                project(i)
+            if step < 68:
+                for i in projected:
+                    project(i)
             for j in ahead[:1] if k == 1 else ahead[1:] if k == 3 else []:
                 bank = acc[projected[0]] if projected else psum_o.tile([P, N_PAD], F32, name="acc")
                 tensor_fold(c + 1, j, bank)

@@ -51,7 +51,7 @@ def vector_tiles(c):
 
 
 def tensor_tiles(c):
-    return [] if c < 3 else [2, 3] if c % 2 and c > 3 else [3]
+    return [] if c < 4 else [2, 3] if c % 2 or c == 8 else [3]
 
 
 def tile_traceableencoderlayer_pa_t_kernel(tc, x, ln1_w, qkv_w, out_0, out_1, out_2):
@@ -90,7 +90,7 @@ def tile_traceableencoderlayer_pa_t_kernel(tc, x, ln1_w, qkv_w, out_0, out_1, ou
             out=gain_rows[0:SLOTS, :].rearrange("m (b r) -> m b r", r=RUN),
             in_=ln1_w.rearrange("(b m r) -> m b r", m=SLOTS, r=RUN),
         )
-        load(1)
+        load(1, parts=((0, 1), (1, 2), (2, 4)))
         w_raw = const.tile([P, C // P, D], BF16, name="w_raw")
         nc.sync.dma_start(out=w_raw[:], in_=qkv_w.rearrange("(a p) k -> p a k", p=P))
 
@@ -260,19 +260,20 @@ def tile_traceableencoderlayer_pa_t_kernel(tc, x, ln1_w, qkv_w, out_0, out_1, ou
                 in_=grouped[c][:, lo:hi, :, :, :].rearrange("p j g r t -> p (j g r t)"),
             )
 
-        def project(i):
+        def project(i, parts):
             c, j = divmod(i, CHUNK)
             acc[i] = psum_o.tile([P, N_PAD], F32, name="acc")
-            for g in range(PASSES):
-                nc.tensor.matmul_mx(
-                    out=acc[i][:],
-                    lhsT=codes[c][:, j, g, :].bitcast(FP8X4),
-                    lhsT_scale=scales[c][:, j, g, :],
-                    rhs=w_codes[:, g, :].bitcast(FP8X4),
-                    rhs_scale=w_scales[:, g, :],
-                    start=(g == 0),
-                    stop=(g == PASSES - 1),
-                )
+            for lo, hi in parts:
+                for g in range(PASSES):
+                    nc.tensor.matmul_mx(
+                        out=acc[i][:, lo:hi],
+                        lhsT=codes[c][:, j, g, :].bitcast(FP8X4),
+                        lhsT_scale=scales[c][:, j, g, :],
+                        rhs=w_codes[:, g, lo:hi].bitcast(FP8X4),
+                        rhs_scale=w_scales[:, g, lo:hi],
+                        start=(g == 0),
+                        stop=(g == PASSES - 1),
+                    )
 
         def copy_out(i):
             c, j = divmod(i, CHUNK)
@@ -298,6 +299,11 @@ def tile_traceableencoderlayer_pa_t_kernel(tc, x, ln1_w, qkv_w, out_0, out_1, ou
 
         def project_lag(i):
             return QUANTISE_LAG if i < TILES - 2 * CHUNK else LAST_QUANTISE_LAG + 1
+
+        def folds_at(step):
+            c, k = step // CHUNK + 1, step % CHUNK
+            tiles = [(c, j) for j in tensor_tiles(c)] if 0 < c < CHUNKS else []
+            return tiles[:1] if k == 1 else tiles[1:] if k == 3 else []
 
         def spread(work, k):
             return [w for m, w in enumerate(work) if m * CHUNK // len(work) == k]
@@ -337,8 +343,6 @@ def tile_traceableencoderlayer_pa_t_kernel(tc, x, ln1_w, qkv_w, out_0, out_1, ou
                 start_moments(0)
             if k == 1 and c + 1 < CHUNKS:
                 start_moments(c + 1)
-            ahead = tensor_tiles(c + 1) if c + 1 < CHUNKS else []
-            here = tensor_tiles(c) if c < CHUNKS else []
             halves = [divmod(m, 2) for m in range(2 * vector_tiles(c))]
             halves = spread(halves, k) if measured else []
 
@@ -373,10 +377,8 @@ def tile_traceableencoderlayer_pa_t_kernel(tc, x, ln1_w, qkv_w, out_0, out_1, ou
                 nc.vector.tensor_copy(out=gain_cols[:].rearrange("p g t -> p (g t)"), in_=gain_turned[:, 0:SLOTS])
                 inverse_deviation(0)
 
-            if k == 2 and ahead:
-                folded_mean(c + 1, ahead[0])
-            if k == 0 and here[1:]:
-                folded_mean(c, here[1])
+            for tile in folds_at(step - 1):
+                folded_mean(*tile)
             passes = spread(scalar_work(c), k) if measured and c < LAST else []
             for j in last_tile(step, NORMALISE_LAG - 2):
                 scalar_deviation(LAST, j, j + 1, 1.0 if j < vector_tiles(LAST) else 1.0 / D)
@@ -400,18 +402,20 @@ def tile_traceableencoderlayer_pa_t_kernel(tc, x, ln1_w, qkv_w, out_0, out_1, ou
             if normalised is not None:
                 normalise(normalised)
 
-            if step >= 68:
+            parts = ((0, 256), (256, C)) if folds_at(step) or step >= 68 else ((0, N_PAD),)
+
+            if step >= 68 or step < 18:
                 for i in projected:
-                    project(i)
+                    project(i, parts)
             if turned_now is not None:
                 for g in range(PASSES):
                     transpose(turned_now, g)
-            if step < 68:
+            if 18 <= step < 68:
                 for i in projected:
-                    project(i)
-            for j in ahead[:1] if k == 1 else ahead[1:] if k == 3 else []:
+                    project(i, parts)
+            for tile in folds_at(step):
                 bank = acc[projected[0]] if projected else psum_o.tile([P, N_PAD], F32, name="acc")
-                tensor_fold(c + 1, j, bank)
+                tensor_fold(*tile, bank)
             for i in copied:
                 if i % CHUNK == CHUNK - 1:
                     store(i // CHUNK)

@@ -91,6 +91,7 @@ def tile_traceableencoderlayer_pa_t_kernel(tc, x, ln1_w, qkv_w, out_0, out_1, ou
             in_=ln1_w.rearrange("(b m r) -> m b r", m=SLOTS, r=RUN),
         )
         load(1, parts=((0, 1), (1, 2), (2, 4)))
+        load(2)
         w_raw = const.tile([P, C // P, D], BF16, name="w_raw")
         nc.sync.dma_start(out=w_raw[:], in_=qkv_w.rearrange("(a p) k -> p a k", p=P))
 
@@ -246,6 +247,15 @@ def tile_traceableencoderlayer_pa_t_kernel(tc, x, ln1_w, qkv_w, out_0, out_1, ou
                 grouped[c] = mx_pool.tile([P, CHUNK, PASSES, P, PACK], BF16, name="grouped", align_bytes=64)
                 codes[c] = mx_pool.tile([P, CHUNK, PASSES, P], U32, name="codes", align_bytes=64)
                 scales[c] = mx_pool.tile([P, CHUNK, PASSES, P], U8, name="scales", align_bytes=64)
+            if i == TILES - 1 and g == 0:
+                for t in range(PACK):
+                    nc.scalar.activation(
+                        out=grouped[c][:, j, g, :, t],
+                        in_=turned[i, g][:, t, :],
+                        func=ACT.Copy,
+                        scale=gain_cols[:, g, t : t + 1],
+                    )
+                return
             nc.vector.tensor_tensor(
                 out=grouped[c][:, j, g, :, :],
                 in0=turned[i, g][:].rearrange("p t r -> p r t"),
@@ -318,7 +328,7 @@ def tile_traceableencoderlayer_pa_t_kernel(tc, x, ln1_w, qkv_w, out_0, out_1, ou
                 squares = squares[1:] + [(scalar_squares, j)]
             return work + squares + [(scalar_squares, j) for j in tensor_tiles(c)[1:]]
 
-        WEIGHTS_STEP = NORMALISE_LAG + 2
+        WEIGHTS_STEP = NORMALISE_LAG + 3
         LAST = CHUNKS - 1
 
         def last_tile(step, lag):
@@ -337,7 +347,7 @@ def tile_traceableencoderlayer_pa_t_kernel(tc, x, ln1_w, qkv_w, out_0, out_1, ou
             projected = [i for i in range(TILES) if i + project_lag(i) == step]
             copied = [i for i in range(TILES) if i + project_lag(i) + 1 == step]
 
-            if k == 0 and c + PREFETCH < CHUNKS:
+            if k == 0 and 2 < c + PREFETCH < CHUNKS:
                 load(c + PREFETCH)
             if step == 0:
                 start_moments(0)
@@ -348,8 +358,12 @@ def tile_traceableencoderlayer_pa_t_kernel(tc, x, ln1_w, qkv_w, out_0, out_1, ou
 
             if gained is not None:
                 gain(gained, 1)
+            if gained is not None and step >= 67:
+                gain(gained, 0)
             if finished:
                 vector_moments(c - 1)
+            if step == QUANTISE_LAG:
+                quantise_weights()
             if quantised is not None and quantised % CHUNK == 0 and quantised < TILES - 2 * CHUNK:
                 quantise(quantised // CHUNK, 0, CHUNK)
             if step - LAST_QUANTISE_LAG - 1 in (TILES - 2 * CHUNK, TILES - 2 * CHUNK + 2):
@@ -364,9 +378,7 @@ def tile_traceableencoderlayer_pa_t_kernel(tc, x, ln1_w, qkv_w, out_0, out_1, ou
                 inverse_deviation(LAST, j, j + 1)
             for j, h in halves[0::2]:
                 vector_statistics(c, j, h)
-            if step == QUANTISE_LAG - 1:
-                quantise_weights()
-            if gained is not None:
+            if gained is not None and not (step >= 67):
                 gain(gained, 0)
             for j, h in halves[1::2]:
                 vector_statistics(c, j, h)

@@ -22,6 +22,7 @@ K_PASS = P * PACK
 PASSES = D // K_PASS
 RUN = 8
 SLOTS = PASSES * PACK
+W_COLUMNS = PASSES * C
 N_PAD = 512
 BN_WIDTH = 512
 BN_DIM = 6
@@ -104,10 +105,11 @@ def tile_traceableencoderlayer_pa_t_kernel(tc, x, ln1_w, qkv_w, out_0, out_1, ou
         sqrt_first = const.tile([P, 1], F32, name="sqrt_first")
         nc.scalar.activation(out=sqrt_first[:], in_=eps[:], func=ACT.Sqrt)
 
-        w_grouped = const.tile([P, PASSES, N_PAD, PACK], BF16, name="w_grouped", align_bytes=64)
-        nc.gpsimd.memset(w_grouped[:, :, C:N_PAD, :], 0.0)
-        w_codes = const.tile([P, PASSES, N_PAD], U32, name="w_codes", align_bytes=64)
-        w_scales = const.tile([P, PASSES, N_PAD], U8, name="w_scales", align_bytes=64)
+        w_grouped = const.tile([P, PASSES, C, PACK], BF16, name="w_grouped", align_bytes=64)
+        w_codes = const.tile([P, W_COLUMNS + N_PAD - C], U32, name="w_codes", align_bytes=64)
+        w_scales = const.tile([P, W_COLUMNS + N_PAD - C], U8, name="w_scales", align_bytes=64)
+        nc.gpsimd.memset(w_codes[:, W_COLUMNS:], 0)
+        nc.gpsimd.memset(w_scales[:, W_COLUMNS:], 0)
         gain_cols = const.tile([P, PASSES, PACK], F32, name="gain_cols")
 
         w_slots = const.tile([P, C // P, SLOTS, P], BF16, name="w_slots")
@@ -130,11 +132,13 @@ def tile_traceableencoderlayer_pa_t_kernel(tc, x, ln1_w, qkv_w, out_0, out_1, ou
             )
 
         def quantise_weights():
-            nc.vector.quantize_mx(
-                out=w_codes[:].rearrange("p g c -> p (g c)").bitcast(FP8X4),
-                scales=w_scales[:].rearrange("p g c -> p (g c)"),
-                in_=w_grouped[:].rearrange("p g c t -> p (g c t)"),
-            )
+            words = w_grouped[:].rearrange("p g c t -> p (g c t)")
+            for lo, hi in ((0, 512), (512, W_COLUMNS)):
+                nc.vector.quantize_mx(
+                    out=w_codes[:, lo:hi].bitcast(FP8X4),
+                    scales=w_scales[:, lo:hi],
+                    in_=words[:, PACK * lo : PACK * hi],
+                )
 
         def start_moments(c):
             moments[c] = stats.tile([P, CHUNK, 2], F32, name="moments")
@@ -279,8 +283,8 @@ def tile_traceableencoderlayer_pa_t_kernel(tc, x, ln1_w, qkv_w, out_0, out_1, ou
                         out=acc[i][:, lo:hi],
                         lhsT=codes[c][:, j, g, :].bitcast(FP8X4),
                         lhsT_scale=scales[c][:, j, g, :],
-                        rhs=w_codes[:, g, lo:hi].bitcast(FP8X4),
-                        rhs_scale=w_scales[:, g, lo:hi],
+                        rhs=w_codes[:, g * C + lo : g * C + hi].bitcast(FP8X4),
+                        rhs_scale=w_scales[:, g * C + lo : g * C + hi],
                         start=(g == 0),
                         stop=(g == PASSES - 1),
                     )
@@ -316,17 +320,17 @@ def tile_traceableencoderlayer_pa_t_kernel(tc, x, ln1_w, qkv_w, out_0, out_1, ou
             return tiles[:1] if k == 1 else tiles[1:] if k == 3 else []
 
         def spread(work, k):
-            return [w for m, w in enumerate(work) if m * CHUNK // len(work) == k]
+            return [w for m, w in enumerate(work) if min(-(-m * CHUNK // len(work)), CHUNK - 1) == k]
 
         def scalar_work(c):
             own = [j for j in range(vector_tiles(c), CHUNK) if j not in tensor_tiles(c)]
             means = [(scalar_mean, j) for j in own]
-            squares = [(scalar_squares, j) for j in tensor_tiles(c)[:1]]
+            squares = []
             work = []
             for mean, j in zip(means, own):
                 work += [mean] + squares[:1]
                 squares = squares[1:] + [(scalar_squares, j)]
-            return work + squares + [(scalar_squares, j) for j in tensor_tiles(c)[1:]]
+            return work + squares + [(scalar_squares, j) for j in tensor_tiles(c)]
 
         WEIGHTS_STEP = NORMALISE_LAG + 3
         LAST = CHUNKS - 1
@@ -376,11 +380,9 @@ def tile_traceableencoderlayer_pa_t_kernel(tc, x, ln1_w, qkv_w, out_0, out_1, ou
                 inverse_deviation(normalised // CHUNK)
             for j in last_tile(step, NORMALISE_LAG):
                 inverse_deviation(LAST, j, j + 1)
-            for j, h in halves[0::2]:
-                vector_statistics(c, j, h)
             if gained is not None and not (step >= 67):
                 gain(gained, 0)
-            for j, h in halves[1::2]:
+            for j, h in halves:
                 vector_statistics(c, j, h)
             if step == MOMENTS_LAG:
                 deviation(0)
@@ -389,8 +391,6 @@ def tile_traceableencoderlayer_pa_t_kernel(tc, x, ln1_w, qkv_w, out_0, out_1, ou
                 nc.vector.tensor_copy(out=gain_cols[:].rearrange("p g t -> p (g t)"), in_=gain_turned[:, 0:SLOTS])
                 inverse_deviation(0)
 
-            for tile in folds_at(step - 1):
-                folded_mean(*tile)
             passes = spread(scalar_work(c), k) if measured and c < LAST else []
             for j in last_tile(step, NORMALISE_LAG - 2):
                 scalar_deviation(LAST, j, j + 1, 1.0 if j < vector_tiles(LAST) else 1.0 / D)
@@ -398,31 +398,33 @@ def tile_traceableencoderlayer_pa_t_kernel(tc, x, ln1_w, qkv_w, out_0, out_1, ou
             passes += [(scalar_squares, j) for j in last_tile(step, NORMALISE_LAG - 3) if j in singles]
             singles = [j for j in singles if j not in tensor_tiles(LAST)]
             passes += [(scalar_mean, j) for j in last_tile(step, NORMALISE_LAG - 4) if j in singles]
-            for scalar_pass, j in passes[0::2]:
-                scalar_pass(min(c, LAST), j)
             for i in copied:
                 copy_out(i)
+            for scalar_pass, j in passes[0::2]:
+                scalar_pass(min(c, LAST), j)
+            for tile in folds_at(step - 1):
+                folded_mean(*tile)
+            if finished and 1 < c <= LAST:
+                deviation(c - 1)
             if step == WEIGHTS_STEP - 2:
                 sort_weights()
             if WEIGHTS_STEP <= step < WEIGHTS_STEP + C // P:
                 group_weights(step - WEIGHTS_STEP)
             for scalar_pass, j in passes[1::2]:
                 scalar_pass(min(c, LAST), j)
-            if finished and 1 < c <= LAST:
-                deviation(c - 1)
 
             if normalised is not None:
                 normalise(normalised)
 
             parts = ((0, 256), (256, C)) if folds_at(step) or step >= 68 else ((0, N_PAD),)
 
-            if step >= 68 or step < 18:
+            if step >= 70 or step < 18:
                 for i in projected:
                     project(i, parts)
             if turned_now is not None:
                 for g in range(PASSES):
                     transpose(turned_now, g)
-            if 18 <= step < 68:
+            if 18 <= step < 70:
                 for i in projected:
                     project(i, parts)
             for tile in folds_at(step):

@@ -84,7 +84,7 @@ def tile_traceableencoderlayer_pa_t_kernel(tc, x, ln1_w, qkv_w, out_0, out_1, ou
                     in_=rows[:, q * CHUNK + lo : q * CHUNK + hi, :],
                 )
 
-        load(0, parts=((0, 1), (3, 4), (1, 2), (2, 3)))
+        load(0, parts=((0, 1), (1, 2), (3, 4), (2, 3)))
         gain_rows = const.tile([P, P], BF16, name="gain_rows")
         nc.gpsimd.memset(gain_rows[:], 0.0)
         nc.sync.dma_start(
@@ -278,9 +278,12 @@ def tile_traceableencoderlayer_pa_t_kernel(tc, x, ln1_w, qkv_w, out_0, out_1, ou
             c, j = divmod(i, CHUNK)
             acc[i] = psum_o.tile([P, N_PAD], F32, name="acc")
             for lo, hi in parts:
+                bank = acc[i]
+                if i == TILES - 1 and lo > 0:
+                    bank = acc[i, "v"] = psum_o.tile([P, N_PAD], F32, name="acc")
                 for g in range(PASSES):
                     nc.tensor.matmul_mx(
-                        out=acc[i][:, lo:hi],
+                        out=bank[:, lo:hi],
                         lhsT=codes[c][:, j, g, :].bitcast(FP8X4),
                         lhsT_scale=scales[c][:, j, g, :],
                         rhs=w_codes[:, g * C + lo : g * C + hi].bitcast(FP8X4),
@@ -293,6 +296,16 @@ def tile_traceableencoderlayer_pa_t_kernel(tc, x, ln1_w, qkv_w, out_0, out_1, ou
             c, j = divmod(i, CHUNK)
             if j == 0:
                 out_tiles[c] = out_pool.tile([P, 3 * HEADS, CHUNK, DH], F32, name="out_chunk")
+            if i == TILES - 1:
+                nc.scalar.copy(
+                    out=out_tiles[c][:, 0:8, j, :],
+                    in_=acc[i][:, 0:256].rearrange("p (a d) -> p a d", d=DH),
+                )
+                nc.vector.tensor_copy(
+                    out=out_tiles[c][:, 8:12, j, :],
+                    in_=acc[i, "v"][:, 256:C].rearrange("p (a d) -> p a d", d=DH),
+                )
+                return
             nc.scalar.copy(
                 out=out_tiles[c][:, :, j, :],
                 in_=acc[i][:, 0:C].rearrange("p (a d) -> p a d", d=DH),
@@ -320,7 +333,7 @@ def tile_traceableencoderlayer_pa_t_kernel(tc, x, ln1_w, qkv_w, out_0, out_1, ou
             return tiles[:1] if k == 1 else tiles[1:] if k == 3 else []
 
         def spread(work, k):
-            return [w for m, w in enumerate(work) if min(-(-m * CHUNK // len(work)), CHUNK - 1) == k]
+            return [w for m, w in enumerate(work) if (2 * m + 1) * CHUNK // (2 * len(work)) == k]
 
         def scalar_work(c):
             own = [j for j in range(vector_tiles(c), CHUNK) if j not in tensor_tiles(c)]

from contextlib import ExitStack

import concourse.mybir as mybir
from concourse.masks import make_identity

BF16 = mybir.dt.bfloat16
F32 = mybir.dt.float32
U32 = mybir.dt.uint32
U8 = mybir.dt.uint8
FP8X4 = mybir.dt.float8_e4m3fn_x4
ALU = mybir.AluOpType
ACT = mybir.ActivationFunctionType

BATCH, TOKENS, D = 4, 2048, 1024
HEADS, DH = 4, 32
C = 3 * HEADS * DH
EPS = 1e-5

P = 128
PACK = 4
K_PASS = P * PACK
PASSES = D // K_PASS
RUN = 8
SLOTS = PASSES * PACK
W_COLUMNS = PASSES * C
N_PAD = 512
BN_WIDTH = 512
BN_DIM = 6

ROWS = TOKENS // P
CHUNK = 4
TILES = BATCH * ROWS
CHUNKS = TILES // CHUNK
CHUNKS_PER_BATCH = ROWS // CHUNK
PREFETCH = 2

MOMENTS_LAG = CHUNK
NORMALISE_LAG = MOMENTS_LAG + CHUNK - 1
TRANSPOSE_LAG = NORMALISE_LAG + 1
GAIN_LAG = TRANSPOSE_LAG + 2
QUANTISE_LAG = GAIN_LAG + CHUNK + 1
LAST_QUANTISE_LAG = GAIN_LAG + 1
COPY_LAG = QUANTISE_LAG + 1

FLOPS = 2 * BATCH * TOKENS * D * C


def vector_tiles(c):
    if c == CHUNKS - 1:
        return 0
    return CHUNK - 1 if c < 2 else 2 if c == 2 else 1


def tensor_tiles(c):
    return [] if c < 4 else [2, 3] if c % 2 or c == 8 else [3]


def tile_traceableencoderlayer_pa_t_kernel(tc, x, ln1_w, qkv_w, out_0, out_1, out_2):
    nc = tc.nc
    outs = (out_0, out_1, out_2)

    with ExitStack() as ctx:
        const = ctx.enter_context(tc.tile_pool(name="const", bufs=1))
        x_pool = ctx.enter_context(tc.tile_pool(name="x_pool", bufs=PREFETCH + 4))
        stats = ctx.enter_context(tc.tile_pool(name="stats", bufs=5))
        scrap = ctx.enter_context(tc.tile_pool(name="scrap", bufs=2))
        y_pool = ctx.enter_context(tc.tile_pool(name="y_pool", bufs=5))
        mx_pool = ctx.enter_context(tc.tile_pool(name="mx_pool", bufs=3))
        out_pool = ctx.enter_context(tc.tile_pool(name="out_pool", bufs=3))
        psum_t = ctx.enter_context(tc.psum_pool(name="psum_t", bufs=5))
        psum_o = ctx.enter_context(tc.psum_pool(name="psum_o", bufs=3))
        ctx.enter_context(tc.manual_schedule())

        x_tiles, bn_parts, moments, neg_mean, std, rstd = {}, {}, {}, {}, {}, {}
        y_tiles, turned, grouped, codes, scales, acc, out_tiles = {}, {}, {}, {}, {}, {}, {}

        def load(c, parts=((0, CHUNK),)):
            b, q = divmod(c, CHUNKS_PER_BATCH)
            x_tiles[c] = x_pool.tile([P, CHUNK, D], BF16, name="x_chunk")
            rows = x[b].rearrange("(p s) k -> p s k", s=ROWS)
            for lo, hi in parts:
                nc.sync.dma_start(
                    out=x_tiles[c][:, lo:hi, :],
                    in_=rows[:, q * CHUNK + lo : q * CHUNK + hi, :],
                )

        load(0, parts=((0, 1), (1, 2), (3, 4), (2, 3)))
        gain_rows = const.tile([P, P], BF16, name="gain_rows")
        nc.gpsimd.memset(gain_rows[:], 0.0)
        nc.sync.dma_start(
            out=gain_rows[0:SLOTS, :].rearrange("m (b r) -> m b r", r=RUN),
            in_=ln1_w.rearrange("(b m r) -> m b r", m=SLOTS, r=RUN),
        )
        load(1, parts=((0, 1), (1, 2), (2, 4)))
        load(2)
        w_raw = const.tile([P, C // P, D], BF16, name="w_raw")
        nc.sync.dma_start(out=w_raw[:], in_=qkv_w.rearrange("(a p) k -> p a k", p=P))

        ident_bf = const.tile([P, P], BF16, name="ident_bf")
        make_identity(nc, ident_bf[:])
        ident_f32 = const.tile([P, P], F32, name="ident_f32")
        make_identity(nc, ident_f32[:])
        eps = const.tile([P, 1], F32, name="eps")
        nc.gpsimd.memset(eps[:], EPS)
        sqrt_first = const.tile([P, 1], F32, name="sqrt_first")
        nc.scalar.activation(out=sqrt_first[:], in_=eps[:], func=ACT.Sqrt)

        w_grouped = const.tile([P, PASSES, C, PACK], BF16, name="w_grouped", align_bytes=64)
        w_codes = const.tile([P, W_COLUMNS + N_PAD - C], U32, name="w_codes", align_bytes=64)
        w_scales = const.tile([P, W_COLUMNS + N_PAD - C], U8, name="w_scales", align_bytes=64)
        nc.gpsimd.memset(w_codes[:, W_COLUMNS:], 0)
        nc.gpsimd.memset(w_scales[:, W_COLUMNS:], 0)
        gain_cols = const.tile([P, PASSES, PACK], F32, name="gain_cols")

        w_slots = const.tile([P, C // P, SLOTS, P], BF16, name="w_slots")

        def sort_weights():
            for a in range(C // P):
                nc.scalar.copy(
                    out=w_slots[:, a, :, :].rearrange("c m (b r) -> c m b r", r=RUN),
                    in_=w_raw[:, a, :].rearrange("c (b m r) -> c m b r", m=SLOTS, r=RUN),
                )

        def group_weights(a):
            w_turned = psum_o.tile([P, PASSES, PACK, P], BF16, name="w_turned", tag="acc")
            for g in range(PASSES):
                for t in range(PACK):
                    nc.tensor.transpose(w_turned[:, g, t, :], w_slots[:, a, PACK * g + t, :], ident_bf[:])
            nc.scalar.copy(
                out=w_grouped[:, :, a * P : (a + 1) * P, :],
                in_=w_turned[:].rearrange("p g t c -> p g c t"),
            )

        def quantise_weights():
            words = w_grouped[:].rearrange("p g c t -> p (g c t)")
            for lo, hi in ((0, 512), (512, W_COLUMNS)):
                nc.vector.quantize_mx(
                    out=w_codes[:, lo:hi].bitcast(FP8X4),
                    scales=w_scales[:, lo:hi],
                    in_=words[:, PACK * lo : PACK * hi],
                )

        def start_moments(c):
            moments[c] = stats.tile([P, CHUNK, 2], F32, name="moments")
            std[c] = stats.tile([P, CHUNK], F32, name="std")
            rstd[c] = stats.tile([P, CHUNK], F32, name="rstd")
            if vector_tiles(c) > 0:
                bn_parts[c] = stats.tile([P, CHUNK, D // BN_WIDTH, BN_DIM], F32, name="bn_parts")

        def vector_statistics(c, j, h):
            nc.vector.bn_stats(
                out=bn_parts[c][:, j, h, :],
                in_=x_tiles[c][:, j, h * BN_WIDTH : (h + 1) * BN_WIDTH],
            )

        def vector_moments(c):
            for j in range(vector_tiles(c)):
                nc.vector.bn_aggr(
                    out=moments[c][:, j, :], in_=bn_parts[c][:, j, :, :].rearrange("p h s -> p (h s)")
                )

        folded = {}

        def tensor_fold(c, j, bank):
            folded[c, j] = bank[:, C:N_PAD]
            for b in range(D // P):
                nc.tensor.matmul(
                    out=folded[c, j],
                    lhsT=ident_bf[:],
                    rhs=x_tiles[c][:, j, b * P : (b + 1) * P],
                    start=(b == 0),
                    stop=(b == D // P - 1),
                )

        def folded_mean(c, j):
            unread = scrap.tile([P, D], BF16, name="unread")
            nc.scalar.activation(
                out=unread[:, 0:P],
                in_=folded[c, j],
                func=ACT.Identity,
                scale=-1.0 / D,
                accum_out=moments[c][:, j, 0:1],
            )

        def scalar_mean(c, j):
            unread = scrap.tile([P, D], BF16, name="unread")
            nc.scalar.activation(
                out=unread[:],
                in_=x_tiles[c][:, j, :],
                func=ACT.Identity,
                scale=-1.0 / D,
                accum_out=moments[c][:, j, 0:1],
            )

        def scalar_squares(c, j):
            unread = scrap.tile([P, D], BF16, name="unread")
            nc.scalar.activation(
                out=unread[:],
                in_=x_tiles[c][:, j, :],
                func=ACT.Square,
                bias=moments[c][:, j, 0:1],
                scale=1.0,
                accum_out=moments[c][:, j, 1:2],
            )

        def scalar_deviation(c, lo, hi, factor):
            nc.scalar.activation(
                out=std[c][:, lo:hi],
                in_=moments[c][:, lo:hi, 1],
                func=ACT.Sqrt,
                bias=eps[:, 0:1],
                scale=factor,
            )

        def deviation(c):
            n = vector_tiles(c)
            if n > 0:
                negate_means(c)
                scalar_deviation(c, 0, n, 1.0)
            scalar_deviation(c, n, CHUNK, 1.0 / D)

        def inverse_deviation(c, lo=0, hi=CHUNK):
            nc.vector.reciprocal(out=rstd[c][:, lo:hi], in_=std[c][:, lo:hi])

        def negate_means(c):
            n = vector_tiles(c)
            neg_mean[c] = stats.tile([P, CHUNK], F32, name="neg_mean")
            nc.scalar.mul(out=neg_mean[c][:, 0:n], in_=moments[c][:, 0:n, 0], mul=-1.0)

        def normalise(i):
            c, j = divmod(i, CHUNK)
            shift = neg_mean[c][:, j : j + 1] if j < vector_tiles(c) else moments[c][:, j, 0:1]
            y_tiles[i] = y_pool.tile([P, PASSES, PACK, P], F32, name="y")
            nc.gpsimd.tensor_scalar(
                out=y_tiles[i][:].rearrange("p g t (b r) -> p (g t) b r", r=RUN),
                in0=x_tiles[c][:, j, :].rearrange("p (b m r) -> p m b r", m=SLOTS, r=RUN),
                scalar1=shift,
                scalar2=rstd[c][:, j : j + 1],
                op0=ALU.add,
                op1=ALU.mult,
            )

        def transpose(i, g):
            turned[i, g] = psum_t.tile([P, PACK, P], F32, name="turned")
            for t in range(PACK):
                nc.tensor.transpose(turned[i, g][:, t, :], y_tiles[i][:, g, t, :], ident_f32[:])

        def gain(i, g):
            c, j = divmod(i, CHUNK)
            if j == 0 and g == 1:
                grouped[c] = mx_pool.tile([P, CHUNK, PASSES, P, PACK], BF16, name="grouped", align_bytes=64)
                codes[c] = mx_pool.tile([P, CHUNK, PASSES, P], U32, name="codes", align_bytes=64)
                scales[c] = mx_pool.tile([P, CHUNK, PASSES, P], U8, name="scales", align_bytes=64)
            if i == TILES - 1 and g == 0:
                for t in range(PACK):
                    nc.scalar.activation(
                        out=grouped[c][:, j, g, :, t],
                        in_=turned[i, g][:, t, :],
                        func=ACT.Copy,
                        scale=gain_cols[:, g, t : t + 1],
                    )
                return
            nc.vector.tensor_tensor(
                out=grouped[c][:, j, g, :, :],
                in0=turned[i, g][:].rearrange("p t r -> p r t"),
                in1=gain_cols[:, g, :].unsqueeze(1).to_broadcast([P, P, PACK]),
                op=ALU.mult,
            )

        def quantise(c, lo, hi):
            nc.vector.quantize_mx(
                out=codes[c][:, lo:hi, :, :].rearrange("p j g r -> p (j g r)").bitcast(FP8X4),
                scales=scales[c][:, lo:hi, :, :].rearrange("p j g r -> p (j g r)"),
                in_=grouped[c][:, lo:hi, :, :, :].rearrange("p j g r t -> p (j g r t)"),
            )

        def project(i, parts):
            c, j = divmod(i, CHUNK)
            acc[i] = psum_o.tile([P, N_PAD], F32, name="acc")
            for lo, hi in parts:
                bank = acc[i]
                if i == TILES - 1 and lo > 0:
                    bank = acc[i, "v"] = psum_o.tile([P, N_PAD], F32, name="acc")
                for g in range(PASSES):
                    nc.tensor.matmul_mx(
                        out=bank[:, lo:hi],
                        lhsT=codes[c][:, j, g, :].bitcast(FP8X4),
                        lhsT_scale=scales[c][:, j, g, :],
                        rhs=w_codes[:, g * C + lo : g * C + hi].bitcast(FP8X4),
                        rhs_scale=w_scales[:, g * C + lo : g * C + hi],
                        start=(g == 0),
                        stop=(g == PASSES - 1),
                    )

        def copy_out(i):
            c, j = divmod(i, CHUNK)
            if j == 0:
                out_tiles[c] = out_pool.tile([P, 3 * HEADS, CHUNK, DH], F32, name="out_chunk")
            if i == TILES - 1:
                nc.scalar.copy(
                    out=out_tiles[c][:, 0:8, j, :],
                    in_=acc[i][:, 0:256].rearrange("p (a d) -> p a d", d=DH),
                )
                nc.vector.tensor_copy(
                    out=out_tiles[c][:, 8:12, j, :],
                    in_=acc[i, "v"][:, 256:C].rearrange("p (a d) -> p a d", d=DH),
                )
                return
            nc.scalar.copy(
                out=out_tiles[c][:, :, j, :],
                in_=acc[i][:, 0:C].rearrange("p (a d) -> p a d", d=DH),
            )

        def store(c):
            b, q = divmod(c, CHUNKS_PER_BATCH)
            for w in range(3):
                rows = outs[w][b].rearrange("n (p s) d -> p n s d", s=ROWS)
                nc.sync.dma_start(
                    out=rows[:, :, q * CHUNK : (q + 1) * CHUNK, :],
                    in_=out_tiles[c][:, w * HEADS : (w + 1) * HEADS, :, :],
                )

        def due(step, lag):
            i = step - lag
            return i if 0 <= i < TILES else None

        def project_lag(i):
            return QUANTISE_LAG if i < TILES - 2 * CHUNK else LAST_QUANTISE_LAG + 1

        def folds_at(step):
            c, k = step // CHUNK + 1, step % CHUNK
            tiles = [(c, j) for j in tensor_tiles(c)] if 0 < c < CHUNKS else []
            return tiles[:1] if k == 1 else tiles[1:] if k == 3 else []

        def spread(work, k):
            return [w for m, w in enumerate(work) if (2 * m + 1) * CHUNK // (2 * len(work)) == k]

        def scalar_work(c):
            own = [j for j in range(vector_tiles(c), CHUNK) if j not in tensor_tiles(c)]
            means = [(scalar_mean, j) for j in own]
            squares = []
            work = []
            for mean, j in zip(means, own):
                work += [mean] + squares[:1]
                squares = squares[1:] + [(scalar_squares, j)]
            return work + squares + [(scalar_squares, j) for j in tensor_tiles(c)]

        WEIGHTS_STEP = NORMALISE_LAG + 3
        LAST = CHUNKS - 1

        def last_tile(step, lag):
            i = due(step, lag)
            return [i % CHUNK] if i is not None and i // CHUNK == LAST else []

        for step in range(TILES + COPY_LAG):
            c, k = divmod(step, CHUNK)
            measured = due(step, 0) is not None
            finished = due(step, MOMENTS_LAG) is not None and k == 0
            normalised = due(step, NORMALISE_LAG)
            turned_now = due(step, TRANSPOSE_LAG)
            gained = due(step, GAIN_LAG)
            quantised = due(step, QUANTISE_LAG)
            quantised_last = due(step, LAST_QUANTISE_LAG)
            projected = [i for i in range(TILES) if i + project_lag(i) == step]
            copied = [i for i in range(TILES) if i + project_lag(i) + 1 == step]

            if k == 0 and 2 < c + PREFETCH < CHUNKS:
                load(c + PREFETCH)
            if step == 0:
                start_moments(0)
            if k == 1 and c + 1 < CHUNKS:
                start_moments(c + 1)
            halves = [divmod(m, 2) for m in range(2 * vector_tiles(c))]
            halves = spread(halves, k) if measured else []

            if gained is not None:
                gain(gained, 1)
            if gained is not None and step >= 67:
                gain(gained, 0)
            if finished:
                vector_moments(c - 1)
            if step == QUANTISE_LAG:
                quantise_weights()
            if quantised is not None and quantised % CHUNK == 0 and quantised < TILES - 2 * CHUNK:
                quantise(quantised // CHUNK, 0, CHUNK)
            if step - LAST_QUANTISE_LAG - 1 in (TILES - 2 * CHUNK, TILES - 2 * CHUNK + 2):
                j = (step - LAST_QUANTISE_LAG - 1) % CHUNK
                quantise(CHUNKS - 2, j, j + 2)
            if quantised_last is not None and quantised_last >= TILES - CHUNK:
                j = quantised_last % CHUNK
                quantise(CHUNKS - 1, j, j + 1)
            if normalised is not None and normalised % CHUNK == 0 and 0 < normalised < LAST * CHUNK:
                inverse_deviation(normalised // CHUNK)
            for j in last_tile(step, NORMALISE_LAG):
                inverse_deviation(LAST, j, j + 1)
            if gained is not None and not (step >= 67):
                gain(gained, 0)
            for j, h in halves:
                vector_statistics(c, j, h)
            if step == MOMENTS_LAG:
                deviation(0)
                gain_turned = psum_t.tile([P, P], BF16, name="gain_turned", tag="turned")
                nc.tensor.transpose(gain_turned[:], gain_rows[:], ident_bf[:])
                nc.vector.tensor_copy(out=gain_cols[:].rearrange("p g t -> p (g t)"), in_=gain_turned[:, 0:SLOTS])
                inverse_deviation(0)

            passes = spread(scalar_work(c), k) if measured and c < LAST else []
            for j in last_tile(step, NORMALISE_LAG - 2):
                scalar_deviation(LAST, j, j + 1, 1.0 if j < vector_tiles(LAST) else 1.0 / D)
            singles = range(vector_tiles(LAST), CHUNK)
            passes += [(scalar_squares, j) for j in last_tile(step, NORMALISE_LAG - 3) if j in singles]
            singles = [j for j in singles if j not in tensor_tiles(LAST)]
            passes += [(scalar_mean, j) for j in last_tile(step, NORMALISE_LAG - 4) if j in singles]
            for i in copied:
                copy_out(i)
            for scalar_pass, j in passes[0::2]:
                scalar_pass(min(c, LAST), j)
            for tile in folds_at(step - 1):
                folded_mean(*tile)
            if finished and 1 < c <= LAST:
                deviation(c - 1)
            if step == WEIGHTS_STEP - 2:
                sort_weights()
            if WEIGHTS_STEP <= step < WEIGHTS_STEP + C // P:
                group_weights(step - WEIGHTS_STEP)
            for scalar_pass, j in passes[1::2]:
                scalar_pass(min(c, LAST), j)

            if normalised is not None:
                normalise(normalised)

            parts = ((0, 256), (256, C)) if folds_at(step) or step >= 68 else ((0, N_PAD),)

            if step >= 70 or step < 18:
                for i in projected:
                    project(i, parts)
            if turned_now is not None:
                for g in range(PASSES):
                    transpose(turned_now, g)
            if 18 <= step < 70:
                for i in projected:
                    project(i, parts)
            for tile in folds_at(step):
                bank = acc[projected[0]] if projected else psum_o.tile([P, N_PAD], F32, name="acc")
                tensor_fold(*tile, bank)
            for i in copied:
                if i % CHUNK == CHUNK - 1:
                    store(i // CHUNK)
